import numpy as np
import ml_dtypes


def mxq(x, axis, fmt="e4m3"):
    dtype, down = {"e4m3": (ml_dtypes.float8_e4m3fn, 7), "e5m2": (ml_dtypes.float8_e5m2, 14)}[fmt]
    v = np.moveaxis(np.asarray(x, np.float32).astype(ml_dtypes.bfloat16).astype(np.float64), axis, -1)
    blocks = v.reshape(v.shape[:-1] + (-1, 32))
    amax = np.abs(blocks).max(-1, keepdims=True)
    byte = np.maximum(np.where(amax > 0, np.frexp(amax)[1] - 1 + 127, 0) - down, 1)
    scale = np.exp2(byte - 127.0)
    codes = (blocks / scale).astype(np.float32).astype(dtype).astype(np.float64)
    return np.moveaxis((codes * scale).reshape(v.shape), -1, axis)


WIDE = False


def mx_kscale(k):
    if not WIDE:
        return np.ones(k)
    levels = np.array([10, -10, 5, -5, 0])
    if k % 512:
        return np.exp2(np.random.permutation(np.resize(levels, k // 32))).repeat(32)
    a = np.empty((k // 512, 16))
    for p in range(k // 512):
        a[p, :8] = np.random.permutation(np.resize(levels, 8))
        for g in range(8):
            far = levels[np.abs(levels - a[p, g]) >= 10]
            a[p, g + 8] = far[np.random.randint(len(far))]
    return np.exp2(a.ravel()).repeat(32)


BF16 = ml_dtypes.bfloat16


def bf(x):
    return np.asarray(x, np.float32).astype(BF16)


def f64(x):
    return np.asarray(x).astype(np.float64)


B, N, C = 8, 512, 512
R = B * N
G = 3 * C


def sigmoid(v):
    return 1.0 / (1.0 + np.exp(-v))


def setup_inputs():
    s = mx_kscale(C)
    s = s / s.max()
    return {"x_proj": bf(np.random.standard_normal((R, G))),
            "annotations": bf(np.random.standard_normal((B, N, C)) * s),
            "recurrent_kernel": bf(np.random.standard_normal((C, G)) / np.sqrt(C) / s[:, None]),
            "bias_h": bf(np.random.standard_normal(G) * 0.3)}


def reference(x_proj, annotations, recurrent_kernel, bias_h):
    b, n, c = annotations.shape
    h = f64(annotations).reshape(-1, c)
    mh = (mxq(h, 1, "e4m3") @ mxq(f64(recurrent_kernel), 0, "e4m3")) + f64(bias_h)
    xz, xr, xh = np.split(f64(x_proj), 3, axis=-1)
    hz, hr, hh_in = np.split(mh, 3, axis=-1)
    z = sigmoid(xz + hz)
    r = sigmoid(xr + hr)
    hh = np.tanh(xh + r * hh_in)
    out = z * h + (1.0 - z) * hh
    return out.reshape(b, n, c)

@@ -1,0 +1,303 @@
+from contextlib import ExitStack
+
+import concourse.mybir as mybir
+from concourse.masks import make_identity
+
+F32 = mybir.dt.float32
+BF16 = mybir.dt.bfloat16
+U32 = mybir.dt.uint32
+U8 = mybir.dt.uint8
+I32 = mybir.dt.int32
+FP8X4 = mybir.dt.float8_e4m3fn_x4
+ALU = mybir.AluOpType
+FN = mybir.ActivationFunctionType
+
+P = 128
+C = 512
+G = 3 * C
+R = 4096
+TPB = 4
+NFC = C // P
+BLOCK = P * TPB
+NBLK = R // BLOCK
+
+FLOPS = 2 * R * C * G
+NT = R // P
+
+
+def tile_gatedgraphconvolution_pb_t_kernel(tc, x_proj, annotations, recurrent_kernel, bias_h, out):
+    nc = tc.nc
+    h_all = annotations.flatten_outer_dims()
+    out_all = out.flatten_outer_dims()
+
+    with ExitStack() as ctx:
+        ctx.enter_context(tc.manual_schedule())
+        const = ctx.enter_context(tc.tile_pool(name="const", bufs=1))
+        xpool = ctx.enter_context(tc.tile_pool(name="xpool", bufs=3))
+        hpool = ctx.enter_context(tc.tile_pool(name="hpool", bufs=4))
+        qpool = ctx.enter_context(tc.tile_pool(name="qpool", bufs=4))
+        work = ctx.enter_context(tc.tile_pool(name="work", bufs=4))
+        opool = ctx.enter_context(tc.tile_pool(name="opool", bufs=3))
+        psum = ctx.enter_context(tc.psum_pool(name="psum", bufs=1))
+
+        h_blks = {}
+        x_blks = {}
+        o_blks = {}
+        st = {}
+
+        def load_h(b):
+            rows = slice(BLOCK * b, BLOCK * b + BLOCK)
+            h_blks[b] = hpool.tile([P, TPB * C], BF16, name="h_blk", tag="h_blk")
+            nc.sync.dma_start(out=h_blks[b][:], in_=h_all[rows, :].rearrange("(p t) c -> p (t c)", t=TPB))
+
+        def load_x(b):
+            src = x_proj[BLOCK * b : BLOCK * b + BLOCK, :].rearrange("(p t) c -> p t c", t=TPB)
+            x_blks[b] = xpool.tile([P, TPB, G], BF16, name="x_blk", tag="x_blk")
+            for half in range(2):
+                ts = slice(2 * half, 2 * half + 2)
+                nc.sync.dma_start(out=x_blks[b][:, ts, :], in_=src[:, ts, :])
+
+        def load_w(g):
+            cs = slice(C * g, C * g + C)
+            for u in range(2):
+                nc.sync.dma_start(
+                    out=w_raw[:, 2 * u : 2 * u + 2, cs],
+                    in_=recurrent_kernel[:, cs].rearrange("(q t) c -> q t c", t=4)[:, 2 * u : 2 * u + 2, :],
+                )
+
+        def regroup_w(g, copy):
+            cs = slice(C * g, C * g + C)
+            copy(out=w_grp[:, cs, :], in_=w_raw[:, :, cs].rearrange("q t c -> q c t"))
+
+        def quantise_w(g):
+            cs = slice(C * g, C * g + C)
+            nc.vector.quantize_mx(
+                out=w_codes[:, cs].bitcast(FP8X4),
+                scales=w_scales[:, cs],
+                in_=w_grp[:, cs, :].rearrange("q c t -> q (c t)"),
+            )
+
+        def x_of(i, g):
+            return x_blks[i // TPB][:, i % TPB, C * g : C * g + C]
+
+        def h_of(i):
+            t = i % TPB
+            return h_blks[i // TPB][:, C * t : C * t + C]
+
+        def flip(src, tag):
+            ps = psum.tile([P, C], F32, name="ps_" + tag, tag=tag)
+            for j in range(NFC):
+                nc.tensor.transpose(ps[:, P * j : P * j + P], src[:, P * j : P * j + P], ident[:])
+            return ps
+
+        def mx_nodes(i, g):
+            cs = slice(C * g, C * g + C)
+            pg = psum.tile([P, C], F32, name="pg", tag="p%d" % g)
+            nc.tensor.matmul_mx(
+                out=pg[:],
+                lhsT=st[("hc", i)][:].bitcast(FP8X4),
+                lhsT_scale=st[("hs", i)][:],
+                rhs=w_codes[:, cs].bitcast(FP8X4),
+                rhs_scale=w_scales[:, cs],
+                start=True,
+                stop=True,
+            )
+            st[("p", g, i)] = pg
+
+        def add_x(i, g):
+            s = work.tile([P, C], F32, name="s", tag="s%d" % g)
+            nc.vector.tensor_tensor(out=s[:], in0=st[("p", g, i)][:], in1=x_of(i, g), op=ALU.add)
+            st[("s", g, i)] = s
+
+        def sigmoid(i, g, bufs):
+            ps = st[("sT", g, i)]
+            s = work.tile([P, C], F32, name="sg", tag="sg%d" % g, bufs=bufs)
+            for fc in range(NFC):
+                fs = slice(P * fc, P * fc + P)
+                nc.scalar.activation(
+                    out=s[:, fs], in_=ps[:, fs], func=FN.Sigmoid, bias=b_col[:, NFC * g + fc : NFC * g + fc + 1]
+                )
+            st[("gT", g, i)] = s
+
+        def ht(i):
+            h_words = h_of(i).bitcast(F32)
+            xt = psum.tile([P, 2, P], F32, name="xt", tag="xt")
+            for u in range(2):
+                nc.tensor.transpose(xt[:, u, :], h_words[:, u : 2 * P : 2], ident[:])
+            st[("xt", i)] = xt
+
+        def ev(i):
+            h_grp = qpool.tile([P, 4 * P], BF16, name="h_grp", tag="h_grp", align_bytes=64)
+            nc.vector.tensor_copy(
+                out=h_grp[:].bitcast(F32).rearrange("q (p u) -> q p u", u=2),
+                in_=st[("xt", i)][:].rearrange("q u p -> q p u"),
+            )
+            st[("grp", i)] = h_grp
+
+        def q(i):
+            h_codes = qpool.tile([P, P], U32, name="h_codes", tag="h_codes", bufs=8, align_bytes=64)
+            h_scales = qpool.tile([P, P], U8, name="h_scales", tag="h_scales", bufs=8, align_bytes=64)
+            nc.vector.quantize_mx(out=h_codes[:].bitcast(FP8X4), scales=h_scales[:], in_=st[("grp", i)][:])
+            st[("hc", i)] = h_codes
+            st[("hs", i)] = h_scales
+
+        def mxr(i):
+            mx_nodes(i, 1)
+
+        def mxz(i):
+            mx_nodes(i, 0)
+
+        def mxc(i):
+            pc = psum.tile([P, C], F32, name="pc", tag="pc")
+            for fc in range(NFC):
+                cs = slice(2 * C + P * fc, 2 * C + P * fc + P)
+                nc.tensor.matmul_mx(
+                    out=pc[:, P * fc : P * fc + P],
+                    lhsT=w_codes[:, cs].bitcast(FP8X4),
+                    lhsT_scale=w_scales[:, cs],
+                    rhs=st[("hc", i)][:].bitcast(FP8X4),
+                    rhs_scale=st[("hs", i)][:],
+                    start=True,
+                    stop=True,
+                )
+            st[("pc", i)] = pc
+
+        def b0(i):
+            add_x(i, 1)
+
+        def a0(i):
+            add_x(i, 0)
+
+        def tb(i):
+            st[("sT", 1, i)] = flip(st[("s", 1, i)], "bt")
+
+        def ta(i):
+            st[("sT", 0, i)] = flip(st[("s", 0, i)], "at")
+
+        def sr(i):
+            sigmoid(i, 1, 4)
+
+        def sz(i):
+            sigmoid(i, 0, 6)
+
+        def m(i):
+            m_t = work.tile([P, C], F32, name="m_t", tag="mT")
+            for fc in range(NFC):
+                fs = slice(P * fc, P * fc + P)
+                nc.vector.scalar_tensor_tensor(
+                    out=m_t[:, fs],
+                    in0=st[("pc", i)][:, fs],
+                    scalar=b_col[:, 2 * NFC + fc : 2 * NFC + fc + 1],
+                    in1=st[("gT", 1, i)][:, fs],
+                    op0=ALU.add,
+                    op1=ALU.mult,
+                )
+            st[("m", i)] = m_t
+
+        def tm(i):
+            mn = psum.tile([P, C], F32, name="mn", tag="mn")
+            nc.tensor.matmul(out=mn[:], lhsT=ident_bf[:], rhs=x_of(i, 2), start=True, stop=False)
+            for j in range(NFC):
+                js = slice(P * j, P * j + P)
+                nc.tensor.matmul(
+                    out=mn[:, js],
+                    lhsT=st[("m", i)][:, js],
+                    rhs=ident[:],
+                    is_transpose=True,
+                    start=False,
+                    stop=(j == NFC - 1),
+                )
+            st[("mn", i)] = mn
+
+        def th(i):
+            cnd = work.tile([P, C], F32, name="cnd", tag="cd", bufs=6)
+            nc.scalar.activation(out=cnd[:], in_=st[("mn", i)][:], func=FN.Tanh)
+            st[("cd", i)] = cnd
+
+        def mix_engine(i):
+            return nc.vector if i >= NT - 2 else nc.gpsimd
+
+        def u(i):
+            u_t = work.tile([P, C], F32, name="u_t", tag="u", bufs=5)
+            mix_engine(i).tensor_tensor(out=u_t[:], in0=h_of(i), in1=st[("cd", i)][:], op=ALU.subtract)
+            st[("u", i)] = u_t
+
+        def tz(i):
+            st[("zn", i)] = flip(st[("gT", 0, i)], "zn")
+
+        def v(i):
+            nc.vector.tensor_tensor(out=st[("u", i)][:], in0=st[("zn", i)][:], in1=st[("u", i)][:], op=ALU.mult)
+
+        def o(i):
+            b = i // TPB
+            t = i % TPB
+            if t == 0:
+                o_blks[b] = opool.tile([P, TPB, C], F32, name="o_blk", tag="o_blk")
+            mix_engine(i).tensor_tensor(out=o_blks[b][:, t, :], in0=st[("u", i)][:], in1=st[("cd", i)][:], op=ALU.add)
+            dst = out_all[BLOCK * b : BLOCK * b + BLOCK, :].rearrange("(p t) c -> p t c", t=TPB)
+            if b == NBLK - 1:
+                nc.sync.dma_start(out=dst[:, t, :], in_=o_blks[b][:, t, :])
+            elif t == TPB - 1:
+                nc.sync.dma_start(out=dst, in_=o_blks[b][:])
+
+        def run(stage, i):
+            if 0 <= i < NT:
+                stage(i)
+
+        b_rows = const.tile([P, P], BF16)
+        nc.vector.memset(b_rows[:].bitcast(I32), 0)
+        nc.scalar.dma_start(out=b_rows[0 : G // P, :], in_=bias_h.rearrange("(j q) -> j q", q=P))
+        ident = const.tile([P, P], F32)
+        make_identity(nc, ident[:])
+        ident_bf = const.tile([P, P], BF16)
+        make_identity(nc, ident_bf[:])
+        w_raw = const.tile([P, 4, G], BF16)
+        w_grp = const.tile([P, G, 4], BF16, align_bytes=64)
+        w_codes = const.tile([P, G], U32, align_bytes=64)
+        w_scales = const.tile([P, G], U8, align_bytes=64)
+        load_w(1)
+        load_h(0)
+        load_w(2)
+        load_w(0)
+        load_x(0)
+        load_h(1)
+        load_x(1)
+        regroup_w(1, nc.vector.tensor_copy)
+        quantise_w(1)
+        b_rows32 = const.tile([P, P], F32)
+        b_col = const.tile([P, G // P], F32)
+
+        for k in range(-3, NT + 5):
+            if k == -1:
+                quantise_w(0)
+                nc.vector.tensor_copy(out=b_rows32[:], in_=b_rows[:])
+                quantise_w(2)
+                b_ps = psum.tile([P, C], F32, name="b_ps", tag="bt")
+                nc.tensor.transpose(b_ps[:, 0:P], b_rows32[:], ident[:])
+            if k == 0:
+                nc.vector.tensor_copy(out=b_col[:], in_=b_ps[:, 0 : G // P])
+            run(ev, k + 2)
+            run(v, k - 4)
+            run(sr, k - 1)
+            run(tm, k - 2)
+            run(tz, k - 3)
+            run(ta, k - 1)
+            run(ht, k + 3)
+            run(th, k - 2)
+            run(u, k - 3)
+            run(b0, k)
+            run(tb, k)
+            run(m, k - 1)
+            run(sz, k - 1)
+            run(a0, k)
+            run(mxr, k + 1)
+            run(mxc, k)
+            run(q, k + 2)
+            if k == -2:
+                regroup_w(2, nc.scalar.copy)
+                regroup_w(0, nc.vector.tensor_copy)
+            run(mxz, k + 1)
+            run(o, k - 4)
+            if (k + 7) % TPB == 0 and 2 <= (k + 7) // TPB < NBLK:
+                load_h((k + 7) // TPB)
+                load_x((k + 7) // TPB)

@@ -17,12 +17,12 @@ C = 512
 G = 3 * C
 R = 4096
 TPB = 4
-NFC = C // P
 BLOCK = P * TPB
 NBLK = R // BLOCK
+NSLOT = TPB * NBLK
+ZG, RG, CG = 0, 1, 2
 
 FLOPS = 2 * R * C * G
-NT = R // P
 
 
 def tile_gatedgraphconvolution_pb_t_kernel(tc, x_proj, annotations, recurrent_kernel, bias_h, out):
@@ -33,10 +33,10 @@ def tile_gatedgraphconvolution_pb_t_kernel(tc, x_proj, annotations, recurrent_ke
     with ExitStack() as ctx:
         ctx.enter_context(tc.manual_schedule())
         const = ctx.enter_context(tc.tile_pool(name="const", bufs=1))
-        xpool = ctx.enter_context(tc.tile_pool(name="xpool", bufs=3))
-        hpool = ctx.enter_context(tc.tile_pool(name="hpool", bufs=4))
-        qpool = ctx.enter_context(tc.tile_pool(name="qpool", bufs=4))
-        work = ctx.enter_context(tc.tile_pool(name="work", bufs=4))
+        xpool = ctx.enter_context(tc.tile_pool(name="xpool", bufs=4))
+        hpool = ctx.enter_context(tc.tile_pool(name="hpool", bufs=5))
+        qpool = ctx.enter_context(tc.tile_pool(name="qpool", bufs=2))
+        work = ctx.enter_context(tc.tile_pool(name="work", bufs=3))
         opool = ctx.enter_context(tc.tile_pool(name="opool", bufs=3))
         psum = ctx.enter_context(tc.psum_pool(name="psum", bufs=1))
 
@@ -50,24 +50,25 @@ def tile_gatedgraphconvolution_pb_t_kernel(tc, x_proj, annotations, recurrent_ke
             h_blks[b] = hpool.tile([P, TPB * C], BF16, name="h_blk", tag="h_blk")
             nc.sync.dma_start(out=h_blks[b][:], in_=h_all[rows, :].rearrange("(p t) c -> p (t c)", t=TPB))
 
-        def load_x(b):
+        def load_x(b, g0, g1):
             src = x_proj[BLOCK * b : BLOCK * b + BLOCK, :].rearrange("(p t) c -> p t c", t=TPB)
-            x_blks[b] = xpool.tile([P, TPB, G], BF16, name="x_blk", tag="x_blk")
-            for half in range(2):
-                ts = slice(2 * half, 2 * half + 2)
-                nc.sync.dma_start(out=x_blks[b][:, ts, :], in_=src[:, ts, :])
+            if b not in x_blks:
+                x_blks[b] = xpool.tile([P, TPB, G], BF16, name="x_blk", tag="x_blk")
+            cs = slice(C * g0, C * g1)
+            nc.sync.dma_start(out=x_blks[b][:, :, cs], in_=src[:, :, cs])
 
         def load_w(g):
             cs = slice(C * g, C * g + C)
-            for u in range(2):
-                nc.sync.dma_start(
-                    out=w_raw[:, 2 * u : 2 * u + 2, cs],
-                    in_=recurrent_kernel[:, cs].rearrange("(q t) c -> q t c", t=4)[:, 2 * u : 2 * u + 2, :],
-                )
+            nc.sync.dma_start(
+                out=w_raw[:, :, cs], in_=recurrent_kernel[:, cs].rearrange("(q t) c -> q t c", t=4)
+            )
 
-        def regroup_w(g, copy):
-            cs = slice(C * g, C * g + C)
-            copy(out=w_grp[:, cs, :], in_=w_raw[:, :, cs].rearrange("q t c -> q c t"))
+        def regroup_w(g, u, copy):
+            cs = slice(C * g + 256 * u, C * g + 256 * u + 256)
+            copy(
+                out=w_grp[:, cs, :].rearrange("q (e p) t -> q e p t", e=2),
+                in_=w_raw[:, :, cs].rearrange("q t (p e) -> q e p t", e=2),
+            )
 
         def quantise_w(g):
             cs = slice(C * g, C * g + C)
@@ -77,227 +78,230 @@ def tile_gatedgraphconvolution_pb_t_kernel(tc, x_proj, annotations, recurrent_ke
                 in_=w_grp[:, cs, :].rearrange("q c t -> q (c t)"),
             )
 
-        def x_of(i, g):
-            return x_blks[i // TPB][:, i % TPB, C * g : C * g + C]
+        def h_of(k, t):
+            return h_blks[k][:, C * t : C * t + C]
 
-        def h_of(i):
-            t = i % TPB
-            return h_blks[i // TPB][:, C * t : C * t + C]
+        def ht(k, i):
+            xt = psum.tile([P, 2, 2 * P], F32, name="xt", tag="xw", bufs=3)
+            for u in range(2):
+                for a in range(2):
+                    words = h_of(k, 2 * i + a).bitcast(F32)
+                    nc.tensor.transpose(xt[:, u, P * a : P * a + P], words[:, u : 2 * P : 2], ident[:])
+            st["xt", k, i] = xt
 
-        def flip(src, tag):
-            ps = psum.tile([P, C], F32, name="ps_" + tag, tag=tag)
-            for j in range(NFC):
-                nc.tensor.transpose(ps[:, P * j : P * j + P], src[:, P * j : P * j + P], ident[:])
-            return ps
+        def ev(k, i):
+            if i == 0:
+                st["grp", k] = qpool.tile([P, 4 * BLOCK], BF16, name="h_grp", tag="h_grp", align_bytes=64)
+            ws = slice(BLOCK * i, BLOCK * i + BLOCK)
+            nc.scalar.copy(
+                out=st["grp", k][:].bitcast(F32)[:, ws].rearrange("q (n u) -> q n u", u=2),
+                in_=st["xt", k, i][:].rearrange("q u n -> q n u"),
+            )
 
-        def mx_nodes(i, g):
-            cs = slice(C * g, C * g + C)
-            pg = psum.tile([P, C], F32, name="pg", tag="p%d" % g)
+        def q(k):
+            hc = qpool.tile([P, BLOCK], U32, name="h_codes", tag="h_codes", align_bytes=64)
+            hs = qpool.tile([P, BLOCK], U8, name="h_scales", tag="h_scales", align_bytes=64)
+            nc.vector.quantize_mx(out=hc[:].bitcast(FP8X4), scales=hs[:], in_=st["grp", k][:])
+            st["hc", k] = hc
+            st["hs", k] = hs
+
+        def xw(k, g, u):
+            words = x_blks[k][:].bitcast(F32)
+            xp = psum.tile([P, BLOCK], F32, name="xp", tag="xw", bufs=3)
+            for t in range(TPB):
+                w0 = 256 * g + P * u
+                nc.tensor.transpose(xp[:, P * t : P * t + P], words[:, t, w0 : w0 + P], ident[:])
+            st["xp", k, g, u] = xp
+
+        def xe(k, g, u):
+            x_t = work.tile([P, BLOCK, 2], BF16, name="x_t", tag="x_t", bufs=8)
+            nc.scalar.copy(
+                out=x_t[:].rearrange("q n e -> q (n e)").bitcast(F32), in_=st["xp", k, g, u][:]
+            )
+            st["xT", k, g, u] = x_t
+
+        def mx(k, g, f):
+            c0 = C * g + P * f
+            pg = psum.tile([P, BLOCK], F32, name="pg", tag="p%d" % g)
             nc.tensor.matmul_mx(
                 out=pg[:],
-                lhsT=st[("hc", i)][:].bitcast(FP8X4),
-                lhsT_scale=st[("hs", i)][:],
-                rhs=w_codes[:, cs].bitcast(FP8X4),
-                rhs_scale=w_scales[:, cs],
+                lhsT=w_codes[:, c0 : c0 + P].bitcast(FP8X4),
+                lhsT_scale=w_scales[:, c0 : c0 + P],
+                rhs=st["hc", k][:].bitcast(FP8X4),
+                rhs_scale=st["hs", k][:],
                 start=True,
                 stop=True,
             )
-            st[("p", g, i)] = pg
+            st["p", k, g, f] = pg
 
-        def add_x(i, g):
-            s = work.tile([P, C], F32, name="s", tag="s%d" % g)
-            nc.vector.tensor_tensor(out=s[:], in0=st[("p", g, i)][:], in1=x_of(i, g), op=ALU.add)
-            st[("s", g, i)] = s
+        def bias_of(g, f):
+            j = 2 * g + f // 2
+            return b_col[:, f % 2, j : j + 1]
 
-        def sigmoid(i, g, bufs):
-            ps = st[("sT", g, i)]
-            s = work.tile([P, C], F32, name="sg", tag="sg%d" % g, bufs=bufs)
-            for fc in range(NFC):
-                fs = slice(P * fc, P * fc + P)
-                nc.scalar.activation(
-                    out=s[:, fs], in_=ps[:, fs], func=FN.Sigmoid, bias=b_col[:, NFC * g + fc : NFC * g + fc + 1]
-                )
-            st[("gT", g, i)] = s
-
-        def ht(i):
-            h_words = h_of(i).bitcast(F32)
-            xt = psum.tile([P, 2, P], F32, name="xt", tag="xt")
-            for u in range(2):
-                nc.tensor.transpose(xt[:, u, :], h_words[:, u : 2 * P : 2], ident[:])
-            st[("xt", i)] = xt
-
-        def ev(i):
-            h_grp = qpool.tile([P, 4 * P], BF16, name="h_grp", tag="h_grp", align_bytes=64)
-            nc.vector.tensor_copy(
-                out=h_grp[:].bitcast(F32).rearrange("q (p u) -> q p u", u=2),
-                in_=st[("xt", i)][:].rearrange("q u p -> q p u"),
+        def add_x(k, g, f):
+            s = work.tile([P, BLOCK], F32, name="s", tag="s%d" % g)
+            nc.vector.scalar_tensor_tensor(
+                out=s[:],
+                in0=st["p", k, g, f][:],
+                scalar=bias_of(g, f),
+                in1=st["xT", k, g, f // 2][:, :, f % 2],
+                op0=ALU.add,
+                op1=ALU.add,
             )
-            st[("grp", i)] = h_grp
+            st["s", k, g, f] = s
 
-        def q(i):
-            h_codes = qpool.tile([P, P], U32, name="h_codes", tag="h_codes", bufs=8, align_bytes=64)
-            h_scales = qpool.tile([P, P], U8, name="h_scales", tag="h_scales", bufs=8, align_bytes=64)
-            nc.vector.quantize_mx(out=h_codes[:].bitcast(FP8X4), scales=h_scales[:], in_=st[("grp", i)][:])
-            st[("hc", i)] = h_codes
-            st[("hs", i)] = h_scales
+        def sigmoid(k, g, f):
+            gate = work.tile([P, BLOCK], F32, name="gate", tag="g%d" % g, bufs=3 if g == RG else 8)
+            nc.scalar.activation(out=gate[:], in_=st["s", k, g, f][:], func=FN.Sigmoid)
+            st["g", k, g, f] = gate
 
-        def mxr(i):
-            mx_nodes(i, 1)
+        def m(k, f):
+            m_t = work.tile([P, BLOCK], F32, name="m_t", tag="m_t", bufs=8)
+            nc.vector.scalar_tensor_tensor(
+                out=m_t[:],
+                in0=st["p", k, CG, f][:],
+                scalar=bias_of(CG, f),
+                in1=st["g", k, RG, f][:],
+                op0=ALU.add,
+                op1=ALU.mult,
+            )
+            st["m", k, f] = m_t
 
-        def mxz(i):
-            mx_nodes(i, 0)
+        def zn(k, t):
+            ps = psum.tile([P, C], F32, name="zn", tag="zn")
+            for f in range(4):
+                fs = slice(P * f, P * f + P)
+                nc.tensor.transpose(ps[:, fs], st["g", k, ZG, f][:, P * t : P * t + P], ident[:])
+            st["zn", k, t] = ps
 
-        def mxc(i):
-            pc = psum.tile([P, C], F32, name="pc", tag="pc")
-            for fc in range(NFC):
-                cs = slice(2 * C + P * fc, 2 * C + P * fc + P)
-                nc.tensor.matmul_mx(
-                    out=pc[:, P * fc : P * fc + P],
-                    lhsT=w_codes[:, cs].bitcast(FP8X4),
-                    lhsT_scale=w_scales[:, cs],
-                    rhs=st[("hc", i)][:].bitcast(FP8X4),
-                    rhs_scale=st[("hs", i)][:],
-                    start=True,
-                    stop=True,
-                )
-            st[("pc", i)] = pc
-
-        def b0(i):
-            add_x(i, 1)
-
-        def a0(i):
-            add_x(i, 0)
-
-        def tb(i):
-            st[("sT", 1, i)] = flip(st[("s", 1, i)], "bt")
-
-        def ta(i):
-            st[("sT", 0, i)] = flip(st[("s", 0, i)], "at")
-
-        def sr(i):
-            sigmoid(i, 1, 4)
-
-        def sz(i):
-            sigmoid(i, 0, 6)
-
-        def m(i):
-            m_t = work.tile([P, C], F32, name="m_t", tag="mT")
-            for fc in range(NFC):
-                fs = slice(P * fc, P * fc + P)
-                nc.vector.scalar_tensor_tensor(
-                    out=m_t[:, fs],
-                    in0=st[("pc", i)][:, fs],
-                    scalar=b_col[:, 2 * NFC + fc : 2 * NFC + fc + 1],
-                    in1=st[("gT", 1, i)][:, fs],
-                    op0=ALU.add,
-                    op1=ALU.mult,
-                )
-            st[("m", i)] = m_t
-
-        def tm(i):
-            mn = psum.tile([P, C], F32, name="mn", tag="mn")
-            nc.tensor.matmul(out=mn[:], lhsT=ident_bf[:], rhs=x_of(i, 2), start=True, stop=False)
-            for j in range(NFC):
-                js = slice(P * j, P * j + P)
+        def mn(k, t):
+            ps = psum.tile([P, C], F32, name="mn", tag="mn")
+            x_h = x_blks[k][:, t, C * CG : C * CG + C]
+            nc.tensor.matmul(
+                out=ps[:].rearrange("n (u e p) -> n u e p", u=2, e=2),
+                lhsT=ident_bf[:],
+                rhs=x_h.rearrange("n (u p e) -> n u e p", u=2, e=2),
+                start=True,
+                stop=False,
+            )
+            for f in range(4):
+                fs = slice(P * f, P * f + P)
                 nc.tensor.matmul(
-                    out=mn[:, js],
-                    lhsT=st[("m", i)][:, js],
+                    out=ps[:, fs],
+                    lhsT=st["m", k, f][:, P * t : P * t + P],
                     rhs=ident[:],
                     is_transpose=True,
                     start=False,
-                    stop=(j == NFC - 1),
+                    stop=(f == 3),
                 )
-            st[("mn", i)] = mn
+            st["mn", k, t] = ps
 
-        def th(i):
-            cnd = work.tile([P, C], F32, name="cnd", tag="cd", bufs=6)
-            nc.scalar.activation(out=cnd[:], in_=st[("mn", i)][:], func=FN.Tanh)
-            st[("cd", i)] = cnd
+        def natural(ps):
+            return ps[:].rearrange("n (u e p) -> n u p e", u=2, e=2)
 
-        def mix_engine(i):
-            return nc.vector if i >= NT - 2 else nc.gpsimd
+        def th(k, t):
+            cnd = work.tile([P, C], F32, name="cnd", tag="cnd", bufs=4)
+            nc.scalar.activation(
+                out=cnd[:].rearrange("n (u p e) -> n u p e", u=2, e=2), in_=natural(st["mn", k, t]), func=FN.Tanh
+            )
+            st["c", k, t] = cnd
 
-        def u(i):
-            u_t = work.tile([P, C], F32, name="u_t", tag="u", bufs=5)
-            mix_engine(i).tensor_tensor(out=u_t[:], in0=h_of(i), in1=st[("cd", i)][:], op=ALU.subtract)
-            st[("u", i)] = u_t
+        def mixer(k):
+            return nc.vector if k == NBLK - 1 else nc.gpsimd
 
-        def tz(i):
-            st[("zn", i)] = flip(st[("gT", 0, i)], "zn")
+        def u_(k, t):
+            u_t = work.tile([P, C], F32, name="u_t", tag="u_t", bufs=4)
+            mixer(k).tensor_tensor(out=u_t[:], in0=h_of(k, t), in1=st["c", k, t][:], op=ALU.subtract)
+            st["u", k, t] = u_t
 
-        def v(i):
-            nc.vector.tensor_tensor(out=st[("u", i)][:], in0=st[("zn", i)][:], in1=st[("u", i)][:], op=ALU.mult)
+        def v(k, t):
+            u_n = st["u", k, t][:].rearrange("n (u p e) -> n u p e", u=2, e=2)
+            nc.vector.tensor_tensor(out=u_n, in0=natural(st["zn", k, t]), in1=u_n, op=ALU.mult)
 
-        def o(i):
-            b = i // TPB
-            t = i % TPB
+        def o(k, t):
             if t == 0:
-                o_blks[b] = opool.tile([P, TPB, C], F32, name="o_blk", tag="o_blk")
-            mix_engine(i).tensor_tensor(out=o_blks[b][:, t, :], in0=st[("u", i)][:], in1=st[("cd", i)][:], op=ALU.add)
-            dst = out_all[BLOCK * b : BLOCK * b + BLOCK, :].rearrange("(p t) c -> p t c", t=TPB)
-            if b == NBLK - 1:
-                nc.sync.dma_start(out=dst[:, t, :], in_=o_blks[b][:, t, :])
+                o_blks[k] = opool.tile([P, TPB, C], F32, name="o_blk", tag="o_blk")
+            mixer(k).tensor_tensor(out=o_blks[k][:, t, :], in0=st["u", k, t][:], in1=st["c", k, t][:], op=ALU.add)
+            dst = out_all[BLOCK * k : BLOCK * k + BLOCK, :].rearrange("(p t) c -> p t c", t=TPB)
+            if k == NBLK - 1:
+                nc.sync.dma_start(out=dst[:, t, :], in_=o_blks[k][:, t, :])
             elif t == TPB - 1:
-                nc.sync.dma_start(out=dst, in_=o_blks[b][:])
+                nc.sync.dma_start(out=dst, in_=o_blks[k][:])
 
-        def run(stage, i):
-            if 0 <= i < NT:
-                stage(i)
+        def run(stage, s, *args):
+            if 0 <= s < NSLOT:
+                stage(s // TPB, *args, s % TPB)
 
-        b_rows = const.tile([P, P], BF16)
-        nc.vector.memset(b_rows[:].bitcast(I32), 0)
-        nc.scalar.dma_start(out=b_rows[0 : G // P, :], in_=bias_h.rearrange("(j q) -> j q", q=P))
         ident = const.tile([P, P], F32)
         make_identity(nc, ident[:])
         ident_bf = const.tile([P, P], BF16)
         make_identity(nc, ident_bf[:])
+        b_rows = const.tile([P, 2 * P], BF16)
+        nc.vector.memset(b_rows[:].bitcast(I32), 0)
         w_raw = const.tile([P, 4, G], BF16)
         w_grp = const.tile([P, G, 4], BF16, align_bytes=64)
         w_codes = const.tile([P, G], U32, align_bytes=64)
         w_scales = const.tile([P, G], U8, align_bytes=64)
-        load_w(1)
+        b_rows32 = const.tile([P, 2, P], F32)
+        b_col = const.tile([P, 2, 6], F32)
         load_h(0)
-        load_w(2)
-        load_w(0)
-        load_x(0)
+        load_w(RG)
+        load_x(0, RG, RG + 1)
+        load_w(ZG)
+        load_x(0, ZG, ZG + 1)
+        load_w(CG)
+        nc.sync.dma_start(out=b_rows[0:6, :], in_=bias_h.rearrange("(j q) -> j q", q=2 * P))
+        load_x(0, CG, CG + 1)
         load_h(1)
-        load_x(1)
-        regroup_w(1, nc.vector.tensor_copy)
-        quantise_w(1)
-        b_rows32 = const.tile([P, P], F32)
-        b_col = const.tile([P, G // P], F32)
+        load_x(1, 0, 3)
 
-        for k in range(-3, NT + 5):
-            if k == -1:
-                quantise_w(0)
-                nc.vector.tensor_copy(out=b_rows32[:], in_=b_rows[:])
-                quantise_w(2)
-                b_ps = psum.tile([P, C], F32, name="b_ps", tag="bt")
-                nc.tensor.transpose(b_ps[:, 0:P], b_rows32[:], ident[:])
-            if k == 0:
-                nc.vector.tensor_copy(out=b_col[:], in_=b_ps[:, 0 : G // P])
-            run(ev, k + 2)
-            run(v, k - 4)
-            run(sr, k - 1)
-            run(tm, k - 2)
-            run(tz, k - 3)
-            run(ta, k - 1)
-            run(ht, k + 3)
-            run(th, k - 2)
-            run(u, k - 3)
-            run(b0, k)
-            run(tb, k)
-            run(m, k - 1)
-            run(sz, k - 1)
-            run(a0, k)
-            run(mxr, k + 1)
-            run(mxc, k)
-            run(q, k + 2)
-            if k == -2:
-                regroup_w(2, nc.scalar.copy)
-                regroup_w(0, nc.vector.tensor_copy)
-            run(mxz, k + 1)
-            run(o, k - 4)
-            if (k + 7) % TPB == 0 and 2 <= (k + 7) // TPB < NBLK:
-                load_h((k + 7) // TPB)
-                load_x((k + 7) // TPB)
+        for s in range(-TPB, NSLOT + TPB + 2):
+            k1, j = divmod(s + TPB, TPB)
+            if s == -TPB:
+                regroup_w(RG, 0, nc.vector.tensor_copy)
+                regroup_w(RG, 1, nc.vector.tensor_copy)
+                quantise_w(RG)
+            if s == -2:
+                nc.vector.tensor_copy(out=b_rows32[:], in_=b_rows[:].rearrange("j (p e) -> j e p", e=2))
+                b_ps = psum.tile([P, C], F32, name="b_ps", tag="zn")
+                for e in range(2):
+                    nc.tensor.transpose(b_ps[:, P * e : P * e + P], b_rows32[:, e, :], ident[:])
+            if j == 0 and 2 <= k1 + 1 < NBLK:
+                load_h(k1 + 1)
+                load_x(k1 + 1, 0, 3)
+            run(add_x, s, RG)
+            run(add_x, s, ZG)
+            run(sigmoid, s, RG)
+            run(v, s - TPB - 1)
+            if k1 < NBLK and j == 2:
+                q(k1)
+            xg, xu = ((RG, 0), (ZG, 0), (RG, 1), (ZG, 1))[j]
+            if k1 < NBLK:
+                xw(k1, xg, xu)
+            run(mn, s - TPB)
+            if k1 < NBLK and j < 2:
+                ht(k1, j)
+            run(th, s - TPB)
+            run(u_, s - TPB)
+            run(sigmoid, s, ZG)
+            if k1 < NBLK and j < 2:
+                ev(k1, j)
+            if k1 < NBLK:
+                xe(k1, xg, xu)
+            if s == -TPB:
+                regroup_w(ZG, 0, nc.vector.tensor_copy)
+                regroup_w(ZG, 1, nc.vector.tensor_copy)
+                quantise_w(ZG)
+            if s == -2:
+                nc.vector.tensor_copy(
+                    out=b_col[:], in_=b_ps[:, 0 : 2 * P].rearrange("p (e j) -> p e j", e=2)[:, :, 0:6]
+                )
+                regroup_w(CG, 0, nc.vector.tensor_copy)
+                regroup_w(CG, 1, nc.scalar.copy)
+                quantise_w(CG)
+            run(mx, s, CG)
+            run(mx, s + 1, RG)
+            run(mx, s + 1, ZG)
+            run(zn, s - TPB)
+            run(m, s)
+            run(o, s - TPB - 1)

@@ -16,10 +16,11 @@ P = 128
 C = 512
 G = 3 * C
 R = 4096
-TPB = 4
-BLOCK = P * TPB
-NBLK = R // BLOCK
-NSLOT = TPB * NBLK
+NF = C // P
+TILES = (4, 4, 4, 4, 4, 4, 4, 4)
+FIRST = tuple(sum(TILES[:k]) for k in range(len(TILES)))
+NBLK = len(TILES)
+NSTEP = NF * NBLK
 ZG, RG, CG = 0, 1, 2
 
 FLOPS = 2 * R * C * G
@@ -37,96 +38,106 @@ def tile_gatedgraphconvolution_pb_t_kernel(tc, x_proj, annotations, recurrent_ke
         hpool = ctx.enter_context(tc.tile_pool(name="hpool", bufs=5))
         qpool = ctx.enter_context(tc.tile_pool(name="qpool", bufs=2))
         work = ctx.enter_context(tc.tile_pool(name="work", bufs=3))
-        opool = ctx.enter_context(tc.tile_pool(name="opool", bufs=3))
+        opool = ctx.enter_context(tc.tile_pool(name="opool", bufs=2))
         psum = ctx.enter_context(tc.psum_pool(name="psum", bufs=1))
 
         h_blks = {}
-        x_blks = {}
+        x_of = {}
         o_blks = {}
         st = {}
 
-        def load_h(b):
-            rows = slice(BLOCK * b, BLOCK * b + BLOCK)
-            h_blks[b] = hpool.tile([P, TPB * C], BF16, name="h_blk", tag="h_blk")
-            nc.sync.dma_start(out=h_blks[b][:], in_=h_all[rows, :].rearrange("(p t) c -> p (t c)", t=TPB))
+        def rows_of(dram, b):
+            rows = slice(P * FIRST[b], P * (FIRST[b] + TILES[b]))
+            return dram[rows, :].rearrange("(p t) c -> p t c", t=TILES[b])
 
-        def load_x(b, g0, g1):
-            src = x_proj[BLOCK * b : BLOCK * b + BLOCK, :].rearrange("(p t) c -> p t c", t=TPB)
-            if b not in x_blks:
-                x_blks[b] = xpool.tile([P, TPB, G], BF16, name="x_blk", tag="x_blk")
-            cs = slice(C * g0, C * g1)
-            nc.sync.dma_start(out=x_blks[b][:, :, cs], in_=src[:, :, cs])
+        def load_h(b):
+            h_blks[b] = hpool.tile([P, TILES[b] * C], BF16, name="h_blk", tag="h_blk")
+            nc.sync.dma_start(out=h_blks[b][:], in_=rows_of(h_all, b).rearrange("p t c -> p (t c)"))
+
+        def load_x(b):
+            x_blk = xpool.tile([P, TILES[b], G], BF16, name="x_blk", tag="x_blk")
+            nc.sync.dma_start(out=x_blk[:], in_=rows_of(x_proj, b))
+            for g in range(3):
+                x_of[b, g] = x_blk[:, :, C * g : C * g + C]
+
+        def load_x_gate(b, g):
+            x_g = const.tile([P, TILES[b], C], BF16, name="x_g", tag="x_g%d%d" % (b, g))
+            nc.sync.dma_start(out=x_g[:], in_=rows_of(x_proj, b)[:, :, C * g : C * g + C])
+            x_of[b, g] = x_g[:]
 
         def load_w(g):
-            cs = slice(C * g, C * g + C)
+            w_raw[g] = const.tile([P, 4, C], BF16, name="w_raw", tag="w_raw%d" % g)
             nc.sync.dma_start(
-                out=w_raw[:, :, cs], in_=recurrent_kernel[:, cs].rearrange("(q t) c -> q t c", t=4)
+                out=w_raw[g][:],
+                in_=recurrent_kernel[:, C * g : C * g + C].rearrange("(q t) c -> q t c", t=4),
             )
+            w_grp[g] = const.tile([P, C, 4], BF16, name="w_grp", tag="w_grp%d" % g, align_bytes=64)
+            w_codes[g] = const.tile([P, C], U32, name="w_codes", tag="w_codes%d" % g, align_bytes=64)
+            w_scales[g] = const.tile([P, C], U8, name="w_scales", tag="w_scales%d" % g, align_bytes=64)
 
         def regroup_w(g, u, copy):
-            cs = slice(C * g + 256 * u, C * g + 256 * u + 256)
+            cs = slice(256 * u, 256 * u + 256)
             copy(
-                out=w_grp[:, cs, :].rearrange("q (e p) t -> q e p t", e=2),
-                in_=w_raw[:, :, cs].rearrange("q t (p e) -> q e p t", e=2),
+                out=w_grp[g][:, cs, :].rearrange("q (e p) t -> q e p t", e=2),
+                in_=w_raw[g][:, :, cs].rearrange("q t (p e) -> q e p t", e=2),
             )
 
-        def quantise_w(g):
-            cs = slice(C * g, C * g + C)
+        def quantise_w(g, u):
+            cs = slice(256 * u, 256 * u + 256)
             nc.vector.quantize_mx(
-                out=w_codes[:, cs].bitcast(FP8X4),
-                scales=w_scales[:, cs],
-                in_=w_grp[:, cs, :].rearrange("q c t -> q (c t)"),
+                out=w_codes[g][:, cs].bitcast(FP8X4),
+                scales=w_scales[g][:, cs],
+                in_=w_grp[g][:, cs, :].rearrange("q c t -> q (c t)"),
             )
 
         def h_of(k, t):
             return h_blks[k][:, C * t : C * t + C]
 
-        def ht(k, i):
-            xt = psum.tile([P, 2, 2 * P], F32, name="xt", tag="xw", bufs=3)
+        def ht(k, t):
+            xt = psum.tile([P, 2, P], F32, name="xt", tag="xw", bufs=3)
+            words = h_of(k, t).bitcast(F32)
             for u in range(2):
-                for a in range(2):
-                    words = h_of(k, 2 * i + a).bitcast(F32)
-                    nc.tensor.transpose(xt[:, u, P * a : P * a + P], words[:, u : 2 * P : 2], ident[:])
-            st["xt", k, i] = xt
+                nc.tensor.transpose(xt[:, u, :], words[:, u : 2 * P : 2], ident[:])
+            st["xt", k, t] = xt
 
-        def ev(k, i):
-            if i == 0:
-                st["grp", k] = qpool.tile([P, 4 * BLOCK], BF16, name="h_grp", tag="h_grp", align_bytes=64)
-            ws = slice(BLOCK * i, BLOCK * i + BLOCK)
+        def ev(k, t):
+            h_grp = qpool.tile([P, 4 * P], BF16, name="h_grp", tag="h_grp", bufs=4, align_bytes=64)
             nc.scalar.copy(
-                out=st["grp", k][:].bitcast(F32)[:, ws].rearrange("q (n u) -> q n u", u=2),
-                in_=st["xt", k, i][:].rearrange("q u n -> q n u"),
+                out=h_grp[:].bitcast(F32).rearrange("q (n u) -> q n u", u=2),
+                in_=st["xt", k, t][:].rearrange("q u n -> q n u"),
+            )
+            st["grp", k, t] = h_grp
+
+        def q(k, t):
+            if t == 0:
+                st["hc", k] = qpool.tile([P, P * TILES[k]], U32, name="h_codes", tag="h_codes", align_bytes=64)
+                st["hs", k] = qpool.tile([P, P * TILES[k]], U8, name="h_scales", tag="h_scales", align_bytes=64)
+            ns = slice(P * t, P * t + P)
+            nc.vector.quantize_mx(
+                out=st["hc", k][:, ns].bitcast(FP8X4), scales=st["hs", k][:, ns], in_=st["grp", k, t][:]
             )
 
-        def q(k):
-            hc = qpool.tile([P, BLOCK], U32, name="h_codes", tag="h_codes", align_bytes=64)
-            hs = qpool.tile([P, BLOCK], U8, name="h_scales", tag="h_scales", align_bytes=64)
-            nc.vector.quantize_mx(out=hc[:].bitcast(FP8X4), scales=hs[:], in_=st["grp", k][:])
-            st["hc", k] = hc
-            st["hs", k] = hs
-
         def xw(k, g, u):
-            words = x_blks[k][:].bitcast(F32)
-            xp = psum.tile([P, BLOCK], F32, name="xp", tag="xw", bufs=3)
-            for t in range(TPB):
-                w0 = 256 * g + P * u
-                nc.tensor.transpose(xp[:, P * t : P * t + P], words[:, t, w0 : w0 + P], ident[:])
+            xp = psum.tile([P, P * TILES[k]], F32, name="xp", tag="xw", bufs=3)
+            for t in range(TILES[k]):
+                words = x_of[k, g][:, t, :].bitcast(F32)
+                nc.tensor.transpose(xp[:, P * t : P * t + P], words[:, P * u : P * u + P], ident[:])
             st["xp", k, g, u] = xp
 
         def xe(k, g, u):
-            x_t = work.tile([P, BLOCK, 2], BF16, name="x_t", tag="x_t", bufs=8)
+            x_t = work.tile([P, P * TILES[k], 2], BF16, name="x_t", tag="x_t", bufs=8)
             nc.scalar.copy(
                 out=x_t[:].rearrange("q n e -> q (n e)").bitcast(F32), in_=st["xp", k, g, u][:]
             )
             st["xT", k, g, u] = x_t
 
         def mx(k, g, f):
-            c0 = C * g + P * f
-            pg = psum.tile([P, BLOCK], F32, name="pg", tag="p%d" % g)
+            cs = slice(P * f, P * f + P)
+            pg = psum.tile([P, P * TILES[k]], F32, name="pg", tag="p%d" % g)
             nc.tensor.matmul_mx(
                 out=pg[:],
-                lhsT=w_codes[:, c0 : c0 + P].bitcast(FP8X4),
-                lhsT_scale=w_scales[:, c0 : c0 + P],
+                lhsT=w_codes[g][:, cs].bitcast(FP8X4),
+                lhsT_scale=w_scales[g][:, cs],
                 rhs=st["hc", k][:].bitcast(FP8X4),
                 rhs_scale=st["hs", k][:],
                 start=True,
@@ -139,7 +150,7 @@ def tile_gatedgraphconvolution_pb_t_kernel(tc, x_proj, annotations, recurrent_ke
             return b_col[:, f % 2, j : j + 1]
 
         def add_x(k, g, f):
-            s = work.tile([P, BLOCK], F32, name="s", tag="s%d" % g)
+            s = work.tile([P, P * TILES[k]], F32, name="s", tag="s%d" % g)
             nc.vector.scalar_tensor_tensor(
                 out=s[:],
                 in0=st["p", k, g, f][:],
@@ -151,12 +162,12 @@ def tile_gatedgraphconvolution_pb_t_kernel(tc, x_proj, annotations, recurrent_ke
             st["s", k, g, f] = s
 
         def sigmoid(k, g, f):
-            gate = work.tile([P, BLOCK], F32, name="gate", tag="g%d" % g, bufs=3 if g == RG else 8)
+            gate = work.tile([P, P * TILES[k]], F32, name="gate", tag="g%d" % g, bufs=3 if g == RG else 8)
             nc.scalar.activation(out=gate[:], in_=st["s", k, g, f][:], func=FN.Sigmoid)
             st["g", k, g, f] = gate
 
         def m(k, f):
-            m_t = work.tile([P, BLOCK], F32, name="m_t", tag="m_t", bufs=8)
+            m_t = work.tile([P, P * TILES[k]], F32, name="m_t", tag="m_t", bufs=8)
             nc.vector.scalar_tensor_tensor(
                 out=m_t[:],
                 in0=st["p", k, CG, f][:],
@@ -168,15 +179,15 @@ def tile_gatedgraphconvolution_pb_t_kernel(tc, x_proj, annotations, recurrent_ke
             st["m", k, f] = m_t
 
         def zn(k, t):
-            ps = psum.tile([P, C], F32, name="zn", tag="zn")
+            ps = psum.tile([P, C], F32, name="zn", tag="p0" if (k, t) == (NBLK - 1, 1) else "zn")
             for f in range(4):
                 fs = slice(P * f, P * f + P)
                 nc.tensor.transpose(ps[:, fs], st["g", k, ZG, f][:, P * t : P * t + P], ident[:])
             st["zn", k, t] = ps
 
         def mn(k, t):
-            ps = psum.tile([P, C], F32, name="mn", tag="mn")
-            x_h = x_blks[k][:, t, C * CG : C * CG + C]
+            ps = psum.tile([P, C], F32, name="mn", tag="p1" if (k, t) == (NBLK - 1, 1) else "mn")
+            x_h = x_of[k, CG][:, t, :]
             nc.tensor.matmul(
                 out=ps[:].rearrange("n (u e p) -> n u e p", u=2, e=2),
                 lhsT=ident_bf[:],
@@ -200,18 +211,18 @@ def tile_gatedgraphconvolution_pb_t_kernel(tc, x_proj, annotations, recurrent_ke
             return ps[:].rearrange("n (u e p) -> n u p e", u=2, e=2)
 
         def th(k, t):
-            cnd = work.tile([P, C], F32, name="cnd", tag="cnd", bufs=4)
+            cnd = work.tile([P, C], F32, name="cnd", tag="cnd", bufs=5)
             nc.scalar.activation(
                 out=cnd[:].rearrange("n (u p e) -> n u p e", u=2, e=2), in_=natural(st["mn", k, t]), func=FN.Tanh
             )
             st["c", k, t] = cnd
 
-        def mixer(k):
-            return nc.vector if k == NBLK - 1 else nc.gpsimd
+        def mixer(k, t):
+            return nc.vector if FIRST[k] + t >= R // P - 3 else nc.gpsimd
 
         def u_(k, t):
             u_t = work.tile([P, C], F32, name="u_t", tag="u_t", bufs=4)
-            mixer(k).tensor_tensor(out=u_t[:], in0=h_of(k, t), in1=st["c", k, t][:], op=ALU.subtract)
+            mixer(k, t).tensor_tensor(out=u_t[:], in0=h_of(k, t), in1=st["c", k, t][:], op=ALU.subtract)
             st["u", k, t] = u_t
 
         def v(k, t):
@@ -220,88 +231,112 @@ def tile_gatedgraphconvolution_pb_t_kernel(tc, x_proj, annotations, recurrent_ke
 
         def o(k, t):
             if t == 0:
-                o_blks[k] = opool.tile([P, TPB, C], F32, name="o_blk", tag="o_blk")
-            mixer(k).tensor_tensor(out=o_blks[k][:, t, :], in0=st["u", k, t][:], in1=st["c", k, t][:], op=ALU.add)
-            dst = out_all[BLOCK * k : BLOCK * k + BLOCK, :].rearrange("(p t) c -> p t c", t=TPB)
+                o_blks[k] = opool.tile([P, TILES[k], C], F32, name="o_blk", tag="o_blk")
+            mixer(k, t).tensor_tensor(out=o_blks[k][:, t, :], in0=st["u", k, t][:], in1=st["c", k, t][:], op=ALU.add)
+            dst = rows_of(out_all, k)
             if k == NBLK - 1:
                 nc.sync.dma_start(out=dst[:, t, :], in_=o_blks[k][:, t, :])
-            elif t == TPB - 1:
+            elif t == TILES[k] - 1:
                 nc.sync.dma_start(out=dst, in_=o_blks[k][:])
 
-        def run(stage, s, *args):
-            if 0 <= s < NSLOT:
-                stage(s // TPB, *args, s % TPB)
+        def chunk(stage, s, *args):
+            if 0 <= s < NSTEP:
+                stage(s // NF, *args, s % NF)
 
+        def next_h(stage, s):
+            k, t = divmod(s, NF)
+            if k + 1 < NBLK and t < TILES[k + 1]:
+                stage(k + 1, t)
+
+        def tile_step(stage, s):
+            k, t = divmod(s - NF, NF)
+            if 0 <= k < NBLK and t < TILES[k]:
+                stage(k, t)
+
+        w_raw, w_grp, w_codes, w_scales = {}, {}, {}, {}
         ident = const.tile([P, P], F32)
         make_identity(nc, ident[:])
         ident_bf = const.tile([P, P], BF16)
         make_identity(nc, ident_bf[:])
         b_rows = const.tile([P, 2 * P], BF16)
         nc.vector.memset(b_rows[:].bitcast(I32), 0)
-        w_raw = const.tile([P, 4, G], BF16)
-        w_grp = const.tile([P, G, 4], BF16, align_bytes=64)
-        w_codes = const.tile([P, G], U32, align_bytes=64)
-        w_scales = const.tile([P, G], U8, align_bytes=64)
+        warm = const.tile([P, 1], F32)
+        nc.vector.memset(warm[:], 0.0)
+        nc.scalar.activation(out=warm[:], in_=warm[:], func=FN.Sigmoid)
         b_rows32 = const.tile([P, 2, P], F32)
         b_col = const.tile([P, 2, 6], F32)
+        nc.scalar.dma_start(out=b_rows[0:6, :], in_=bias_h.rearrange("(j q) -> j q", q=2 * P))
         load_h(0)
         load_w(RG)
-        load_x(0, RG, RG + 1)
-        load_w(ZG)
-        load_x(0, ZG, ZG + 1)
+        load_x_gate(0, RG)
         load_w(CG)
-        nc.sync.dma_start(out=b_rows[0:6, :], in_=bias_h.rearrange("(j q) -> j q", q=2 * P))
-        load_x(0, CG, CG + 1)
+        load_w(ZG)
+        load_x_gate(0, ZG)
+        load_x_gate(0, CG)
         load_h(1)
-        load_x(1, 0, 3)
+        load_x_gate(1, RG)
+        load_x_gate(1, ZG)
+        load_x_gate(1, CG)
+        for t in range(TILES[0]):
+            ht(0, t)
+            ev(0, t)
+        regroup_w(RG, 0, nc.vector.tensor_copy)
+        for t in range(TILES[0]):
+            q(0, t)
+        quantise_w(RG, 0)
+        regroup_w(RG, 1, nc.vector.tensor_copy)
+        quantise_w(RG, 1)
+        for u in range(2):
+            xw(0, RG, u)
+            xe(0, RG, u)
+        mx(0, RG, 0)
+        nc.vector.tensor_copy(out=b_rows32[:], in_=b_rows[:].rearrange("j (p e) -> j e p", e=2))
+        b_ps = psum.tile([P, C], F32, name="b_ps", tag="zn")
+        for e in range(2):
+            nc.tensor.transpose(b_ps[:, P * e : P * e + P], b_rows32[:, e, :], ident[:])
+        regroup_w(CG, 0, nc.vector.tensor_copy)
+        nc.vector.tensor_copy(out=b_col[:], in_=b_ps[:, 0 : 2 * P].rearrange("p (e j) -> p e j", e=2)[:, :, 0:6])
+        quantise_w(CG, 0)
+        regroup_w(CG, 1, nc.scalar.copy)
+        mx(0, CG, 0)
+        regroup_w(ZG, 0, nc.vector.tensor_copy)
+        quantise_w(ZG, 0)
+        regroup_w(ZG, 1, nc.scalar.copy)
+        quantise_w(CG, 1)
+        quantise_w(ZG, 1)
+        for u in range(2):
+            xw(0, ZG, u)
+            xe(0, ZG, u)
+        mx(0, ZG, 0)
 
-        for s in range(-TPB, NSLOT + TPB + 2):
-            k1, j = divmod(s + TPB, TPB)
-            if s == -TPB:
-                regroup_w(RG, 0, nc.vector.tensor_copy)
-                regroup_w(RG, 1, nc.vector.tensor_copy)
-                quantise_w(RG)
-            if s == -2:
-                nc.vector.tensor_copy(out=b_rows32[:], in_=b_rows[:].rearrange("j (p e) -> j e p", e=2))
-                b_ps = psum.tile([P, C], F32, name="b_ps", tag="zn")
-                for e in range(2):
-                    nc.tensor.transpose(b_ps[:, P * e : P * e + P], b_rows32[:, e, :], ident[:])
-            if j == 0 and 2 <= k1 + 1 < NBLK:
-                load_h(k1 + 1)
-                load_x(k1 + 1, 0, 3)
-            run(add_x, s, RG)
-            run(add_x, s, ZG)
-            run(sigmoid, s, RG)
-            run(v, s - TPB - 1)
-            if k1 < NBLK and j == 2:
-                q(k1)
+        ht(1, 0)
+        ev(1, 0)
+
+        for s in range(NSTEP + NF + 3):
+            k1, j = s // NF + 1, s % NF
             xg, xu = ((RG, 0), (ZG, 0), (RG, 1), (ZG, 1))[j]
+            if j == 0 and k1 + 1 < NBLK:
+                load_h(k1 + 1)
+                load_x(k1 + 1)
+            chunk(add_x, s, RG)
+            chunk(add_x, s, ZG)
+            next_h(q, s)
+            tile_step(th, s - 1)
+            chunk(sigmoid, s, RG)
+            tile_step(v, s - 2)
+            tile_step(u_, s - 1)
             if k1 < NBLK:
                 xw(k1, xg, xu)
-            run(mn, s - TPB)
-            if k1 < NBLK and j < 2:
-                ht(k1, j)
-            run(th, s - TPB)
-            run(u_, s - TPB)
-            run(sigmoid, s, ZG)
-            if k1 < NBLK and j < 2:
-                ev(k1, j)
+            next_h(ht, s + 1)
+            if s > 0:
+                chunk(mx, s, CG)
+            chunk(mx, s + 1, RG)
+            chunk(mx, s + 1, ZG)
+            tile_step(mn, s)
+            tile_step(zn, s - 1)
+            chunk(sigmoid, s, ZG)
             if k1 < NBLK:
                 xe(k1, xg, xu)
-            if s == -TPB:
-                regroup_w(ZG, 0, nc.vector.tensor_copy)
-                regroup_w(ZG, 1, nc.vector.tensor_copy)
-                quantise_w(ZG)
-            if s == -2:
-                nc.vector.tensor_copy(
-                    out=b_col[:], in_=b_ps[:, 0 : 2 * P].rearrange("p (e j) -> p e j", e=2)[:, :, 0:6]
-                )
-                regroup_w(CG, 0, nc.vector.tensor_copy)
-                regroup_w(CG, 1, nc.scalar.copy)
-                quantise_w(CG)
-            run(mx, s, CG)
-            run(mx, s + 1, RG)
-            run(mx, s + 1, ZG)
-            run(zn, s - TPB)
-            run(m, s)
-            run(o, s - TPB - 1)
+            next_h(ev, s + 1)
+            chunk(m, s)
+            tile_step(o, s - 2)

@@ -55,7 +55,7 @@ def tile_gatedgraphconvolution_pb_t_kernel(tc, x_proj, annotations, recurrent_ke
             nc.sync.dma_start(out=h_blks[b][:], in_=rows_of(h_all, b).rearrange("p t c -> p (t c)"))
 
         def load_x(b):
-            x_blk = xpool.tile([P, TILES[b], G], BF16, name="x_blk", tag="x_blk")
+            x_blk = xpool.tile([P, TILES[b], G], BF16, name="x_blk", tag="x_blk", align_bytes=64)
             nc.sync.dma_start(out=x_blk[:], in_=rows_of(x_proj, b))
             for g in range(3):
                 x_of[b, g] = x_blk[:, :, C * g : C * g + C]
@@ -66,20 +66,18 @@ def tile_gatedgraphconvolution_pb_t_kernel(tc, x_proj, annotations, recurrent_ke
             x_of[b, g] = x_g[:]
 
         def load_w(g):
-            w_raw[g] = const.tile([P, 4, C], BF16, name="w_raw", tag="w_raw%d" % g)
             nc.sync.dma_start(
-                out=w_raw[g][:],
+                out=w_raw[:, g, :, :],
                 in_=recurrent_kernel[:, C * g : C * g + C].rearrange("(q t) c -> q t c", t=4),
             )
-            w_grp[g] = const.tile([P, C, 4], BF16, name="w_grp", tag="w_grp%d" % g, align_bytes=64)
             w_codes[g] = const.tile([P, C], U32, name="w_codes", tag="w_codes%d" % g, align_bytes=64)
             w_scales[g] = const.tile([P, C], U8, name="w_scales", tag="w_scales%d" % g, align_bytes=64)
 
         def regroup_w(g, u, copy):
             cs = slice(256 * u, 256 * u + 256)
             copy(
-                out=w_grp[g][:, cs, :].rearrange("q (e p) t -> q e p t", e=2),
-                in_=w_raw[g][:, :, cs].rearrange("q t (p e) -> q e p t", e=2),
+                out=w_grp[:, g, cs, :].rearrange("q (e p) t -> q e p t", e=2),
+                in_=w_raw[:, g, :, cs].rearrange("q t (p e) -> q e p t", e=2),
             )
 
         def quantise_w(g, u):
@@ -87,7 +85,7 @@ def tile_gatedgraphconvolution_pb_t_kernel(tc, x_proj, annotations, recurrent_ke
             nc.vector.quantize_mx(
                 out=w_codes[g][:, cs].bitcast(FP8X4),
                 scales=w_scales[g][:, cs],
-                in_=w_grp[g][:, cs, :].rearrange("q c t -> q (c t)"),
+                in_=w_grp[:, g, cs, :].rearrange("q c t -> q (c t)"),
             )
 
         def h_of(k, t):
@@ -162,12 +160,12 @@ def tile_gatedgraphconvolution_pb_t_kernel(tc, x_proj, annotations, recurrent_ke
             st["s", k, g, f] = s
 
         def sigmoid(k, g, f):
-            gate = work.tile([P, P * TILES[k]], F32, name="gate", tag="g%d" % g, bufs=3 if g == RG else 8)
+            gate = work.tile([P, P * TILES[k]], F32, name="gate", tag="g%d" % g, bufs=3 if g == RG else 10)
             nc.scalar.activation(out=gate[:], in_=st["s", k, g, f][:], func=FN.Sigmoid)
             st["g", k, g, f] = gate
 
         def m(k, f):
-            m_t = work.tile([P, P * TILES[k]], F32, name="m_t", tag="m_t", bufs=8)
+            m_t = work.tile([P, P * TILES[k]], F32, name="m_t", tag="m_t", bufs=9)
             nc.vector.scalar_tensor_tensor(
                 out=m_t[:],
                 in0=st["p", k, CG, f][:],
@@ -253,19 +251,21 @@ def tile_gatedgraphconvolution_pb_t_kernel(tc, x_proj, annotations, recurrent_ke
             if 0 <= k < NBLK and t < TILES[k]:
                 stage(k, t)
 
-        w_raw, w_grp, w_codes, w_scales = {}, {}, {}, {}
+        w_codes, w_scales = {}, {}
+        w_raw = xpool.tile([P, 3, 4, C], BF16, name="w_raw", tag="x_blk", align_bytes=64)
+        w_grp = xpool.tile([P, 3, C, 4], BF16, name="w_grp", tag="x_blk", align_bytes=64)
+        b_rows = const.tile([P, 2 * P], BF16)
+        nc.vector.memset(b_rows[:].bitcast(I32), 0)
         ident = const.tile([P, P], F32)
         make_identity(nc, ident[:])
         ident_bf = const.tile([P, P], BF16)
         make_identity(nc, ident_bf[:])
-        b_rows = const.tile([P, 2 * P], BF16)
-        nc.vector.memset(b_rows[:].bitcast(I32), 0)
+        nc.scalar.dma_start(out=b_rows[0:6, :], in_=bias_h.rearrange("(j q) -> j q", q=2 * P))
         warm = const.tile([P, 1], F32)
         nc.vector.memset(warm[:], 0.0)
         nc.scalar.activation(out=warm[:], in_=warm[:], func=FN.Sigmoid)
         b_rows32 = const.tile([P, 2, P], F32)
         b_col = const.tile([P, 2, 6], F32)
-        nc.scalar.dma_start(out=b_rows[0:6, :], in_=bias_h.rearrange("(j q) -> j q", q=2 * P))
         load_h(0)
         load_w(RG)
         load_x_gate(0, RG)

@@ -177,14 +177,15 @@ def tile_gatedgraphconvolution_pb_t_kernel(tc, x_proj, annotations, recurrent_ke
             st["m", k, f] = m_t
 
         def zn(k, t):
-            ps = psum.tile([P, C], F32, name="zn", tag="p0" if (k, t) == (NBLK - 1, 1) else "zn")
+            ps = psum.tile([P, C], F32, name="zn", tag=("p0", "p1", "p2", "zn")[t] if k == NBLK - 1 else "zn")
             for f in range(4):
                 fs = slice(P * f, P * f + P)
                 nc.tensor.transpose(ps[:, fs], st["g", k, ZG, f][:, P * t : P * t + P], ident[:])
             st["zn", k, t] = ps
 
         def mn(k, t):
-            ps = psum.tile([P, C], F32, name="mn", tag="p1" if (k, t) == (NBLK - 1, 1) else "mn")
+            in_tail = k == NBLK - 1 and t < 3
+            ps = psum.tile([P, C], F32, name="mn", tag="xw" if in_tail else "mn", bufs=3 if in_tail else 1)
             x_h = x_of[k, CG][:, t, :]
             nc.tensor.matmul(
                 out=ps[:].rearrange("n (u e p) -> n u e p", u=2, e=2),
@@ -215,27 +216,60 @@ def tile_gatedgraphconvolution_pb_t_kernel(tc, x_proj, annotations, recurrent_ke
             )
             st["c", k, t] = cnd
 
-        def mixer(k, t):
-            return nc.vector if FIRST[k] + t >= R // P - 3 else nc.gpsimd
-
         def u_(k, t):
             u_t = work.tile([P, C], F32, name="u_t", tag="u_t", bufs=4)
-            mixer(k, t).tensor_tensor(out=u_t[:], in0=h_of(k, t), in1=st["c", k, t][:], op=ALU.subtract)
+            nc.gpsimd.tensor_tensor(out=u_t[:], in0=h_of(k, t), in1=st["c", k, t][:], op=ALU.subtract)
             st["u", k, t] = u_t
 
         def v(k, t):
             u_n = st["u", k, t][:].rearrange("n (u p e) -> n u p e", u=2, e=2)
             nc.vector.tensor_tensor(out=u_n, in0=natural(st["zn", k, t]), in1=u_n, op=ALU.mult)
 
-        def o(k, t):
-            if t == 0:
-                o_blks[k] = opool.tile([P, TILES[k], C], F32, name="o_blk", tag="o_blk")
-            mixer(k, t).tensor_tensor(out=o_blks[k][:, t, :], in0=st["u", k, t][:], in1=st["c", k, t][:], op=ALU.add)
+        def store(k, t):
             dst = rows_of(out_all, k)
             if k == NBLK - 1:
                 nc.sync.dma_start(out=dst[:, t, :], in_=o_blks[k][:, t, :])
             elif t == TILES[k] - 1:
                 nc.sync.dma_start(out=dst, in_=o_blks[k][:])
+
+        def o_of(k, t):
+            if t == 0:
+                o_blks[k] = opool.tile([P, TILES[k], C], F32, name="o_blk", tag="o_blk")
+            return o_blks[k][:, t, :]
+
+        def o(k, t):
+            nc.gpsimd.tensor_tensor(out=o_of(k, t), in0=st["u", k, t][:], in1=st["c", k, t][:], op=ALU.add)
+            store(k, t)
+
+        def th_last(k, t):
+            cnd = work.tile([P, C], F32, name="cnd", tag="cnd", bufs=5)
+            nc.scalar.activation(out=cnd[:], in_=st["mn", k, t][:], func=FN.Tanh)
+            st["c", k, t] = cnd
+
+        def zh(k, t):
+            w = work.tile([P, C], F32, name="zh", tag="u_t", bufs=4)
+            nc.vector.tensor_tensor(
+                out=w[:].rearrange("n (u e p) -> n u e p", u=2, e=2),
+                in0=st["zn", k, t][:].rearrange("n (u e p) -> n u e p", u=2, e=2),
+                in1=h_of(k, t).rearrange("n (u p e) -> n u e p", u=2, e=2),
+                op=ALU.mult,
+            )
+            st["u", k, t] = w
+
+        def zc(k, t):
+            c_t = st["c", k, t]
+            nc.vector.scalar_tensor_tensor(
+                out=c_t[:], in0=st["zn", k, t][:], scalar=1.0, in1=c_t[:], op0=ALU.subtract, op1=ALU.mult
+            )
+
+        def o_last(k, t, engine):
+            engine.tensor_tensor(
+                out=o_of(k, t).rearrange("n (u p e) -> n u p e", u=2, e=2),
+                in0=natural(st["u", k, t]),
+                in1=natural(st["c", k, t]),
+                op=ALU.subtract,
+            )
+            store(k, t)
 
         def chunk(stage, s, *args):
             if 0 <= s < NSTEP:
@@ -260,7 +294,7 @@ def tile_gatedgraphconvolution_pb_t_kernel(tc, x_proj, annotations, recurrent_ke
         make_identity(nc, ident[:])
         ident_bf = const.tile([P, P], BF16)
         make_identity(nc, ident_bf[:])
-        nc.scalar.dma_start(out=b_rows[0:6, :], in_=bias_h.rearrange("(j q) -> j q", q=2 * P))
+        nc.sync.dma_start(out=b_rows[0:6, :], in_=bias_h.rearrange("(j q) -> j q", q=2 * P))
         warm = const.tile([P, 1], F32)
         nc.vector.memset(warm[:], 0.0)
         nc.scalar.activation(out=warm[:], in_=warm[:], func=FN.Sigmoid)
@@ -312,7 +346,7 @@ def tile_gatedgraphconvolution_pb_t_kernel(tc, x_proj, annotations, recurrent_ke
         ht(1, 0)
         ev(1, 0)
 
-        for s in range(NSTEP + NF + 3):
+        for s in range(NSTEP):
             k1, j = s // NF + 1, s % NF
             xg, xu = ((RG, 0), (ZG, 0), (RG, 1), (ZG, 1))[j]
             if j == 0 and k1 + 1 < NBLK:
@@ -340,3 +374,36 @@ def tile_gatedgraphconvolution_pb_t_kernel(tc, x_proj, annotations, recurrent_ke
             next_h(ev, s + 1)
             chunk(m, s)
             tile_step(o, s - 2)
+
+        last = NBLK - 1
+        th_last(last - 1, 3)
+        v(last - 1, 2)
+        o(last - 1, 2)
+        mn(last, 0)
+        zn(last, 0)
+        th_last(last, 0)
+        zh(last, 0)
+        zn(last - 1, 3)
+        mn(last, 1)
+        zn(last, 1)
+        th_last(last, 1)
+        zh(last - 1, 3)
+        zh(last, 1)
+        zc(last, 0)
+        zc(last - 1, 3)
+        mn(last, 2)
+        zn(last, 2)
+        th_last(last, 2)
+        o_last(last, 0, nc.vector)
+        o_last(last - 1, 3, nc.gpsimd)
+        zc(last, 1)
+        zh(last, 2)
+        mn(last, 3)
+        zn(last, 3)
+        th_last(last, 3)
+        o_last(last, 1, nc.vector)
+        zc(last, 2)
+        zh(last, 3)
+        o_last(last, 2, nc.vector)
+        zc(last, 3)
+        o_last(last, 3, nc.vector)

@@ -32,7 +32,6 @@ def tile_gatedgraphconvolution_pb_t_kernel(tc, x_proj, annotations, recurrent_ke
     out_all = out.flatten_outer_dims()
 
     with ExitStack() as ctx:
-        ctx.enter_context(tc.manual_schedule())
         const = ctx.enter_context(tc.tile_pool(name="const", bufs=1))
         xpool = ctx.enter_context(tc.tile_pool(name="xpool", bufs=4))
         hpool = ctx.enter_context(tc.tile_pool(name="hpool", bufs=5))

@@ -91,7 +91,7 @@ def tile_gatedgraphconvolution_pb_t_kernel(tc, x_proj, annotations, recurrent_ke
             return h_blks[k][:, C * t : C * t + C]
 
         def ht(k, t):
-            xt = psum.tile([P, 2, P], F32, name="xt", tag="xw", bufs=3)
+            xt = psum.tile([P, 2, P], F32, name="xt", tag="bank", bufs=8)
             words = h_of(k, t).bitcast(F32)
             for u in range(2):
                 nc.tensor.transpose(xt[:, u, :], words[:, u : 2 * P : 2], ident[:])
@@ -115,7 +115,7 @@ def tile_gatedgraphconvolution_pb_t_kernel(tc, x_proj, annotations, recurrent_ke
             )
 
         def xw(k, g, u):
-            xp = psum.tile([P, P * TILES[k]], F32, name="xp", tag="xw", bufs=3)
+            xp = psum.tile([P, P * TILES[k]], F32, name="xp", tag="bank", bufs=8)
             for t in range(TILES[k]):
                 words = x_of[k, g][:, t, :].bitcast(F32)
                 nc.tensor.transpose(xp[:, P * t : P * t + P], words[:, P * u : P * u + P], ident[:])
@@ -130,7 +130,7 @@ def tile_gatedgraphconvolution_pb_t_kernel(tc, x_proj, annotations, recurrent_ke
 
         def mx(k, g, f):
             cs = slice(P * f, P * f + P)
-            pg = psum.tile([P, P * TILES[k]], F32, name="pg", tag="p%d" % g)
+            pg = psum.tile([P, P * TILES[k]], F32, name="pg", tag="bank", bufs=8)
             nc.tensor.matmul_mx(
                 out=pg[:],
                 lhsT=w_codes[g][:, cs].bitcast(FP8X4),
@@ -159,7 +159,7 @@ def tile_gatedgraphconvolution_pb_t_kernel(tc, x_proj, annotations, recurrent_ke
             st["s", k, g, f] = s
 
         def sigmoid(k, g, f):
-            gate = work.tile([P, P * TILES[k]], F32, name="gate", tag="g%d" % g, bufs=3 if g == RG else 10)
+            gate = work.tile([P, P * TILES[k]], F32, name="gate", tag="g%d" % g, bufs=3 if g == RG else 11)
             nc.scalar.activation(out=gate[:], in_=st["s", k, g, f][:], func=FN.Sigmoid)
             st["g", k, g, f] = gate
 
@@ -176,16 +176,23 @@ def tile_gatedgraphconvolution_pb_t_kernel(tc, x_proj, annotations, recurrent_ke
             st["m", k, f] = m_t
 
         def zn(k, t):
-            ps = psum.tile([P, C], F32, name="zn", tag=("p0", "p1", "p2", "zn")[t] if k == NBLK - 1 else "zn")
+            ps = psum.tile([P, C], F32, name="zn", tag="bank", bufs=8)
             for f in range(4):
                 fs = slice(P * f, P * f + P)
                 nc.tensor.transpose(ps[:, fs], st["g", k, ZG, f][:, P * t : P * t + P], ident[:])
             st["zn", k, t] = ps
 
+        def x_on_vector(k, t):
+            return t in (0, 2) and k < NBLK - 1
+
         def mn(k, t):
-            in_tail = k == NBLK - 1 and t < 3
-            ps = psum.tile([P, C], F32, name="mn", tag="xw" if in_tail else "mn", bufs=3 if in_tail else 1)
+            ps = psum.tile([P, C], F32, name="mn", tag="bank", bufs=8)
             x_h = x_of[k, CG][:, t, :]
+            if x_on_vector(k, t):
+                for f in range(NF):
+                    nc.tensor.transpose(ps[:, P * f : P * f + P], st["m", k, f][:, P * t : P * t + P], ident[:])
+                st["mn", k, t] = ps
+                return
             nc.tensor.matmul(
                 out=ps[:].rearrange("n (u e p) -> n u e p", u=2, e=2),
                 lhsT=ident_bf[:],
@@ -208,15 +215,27 @@ def tile_gatedgraphconvolution_pb_t_kernel(tc, x_proj, annotations, recurrent_ke
         def natural(ps):
             return ps[:].rearrange("n (u e p) -> n u p e", u=2, e=2)
 
+        def ax(k, t):
+            if x_on_vector(k, t):
+                a_t = work.tile([P, C], F32, name="a_t", tag="a_t", bufs=2)
+                a_n = a_t[:].rearrange("n (u p e) -> n u p e", u=2, e=2)
+                x_n = x_of[k, CG][:, t, :].rearrange("n (u p e) -> n u p e", u=2, e=2)
+                nc.vector.tensor_tensor(out=a_n, in0=natural(st["mn", k, t]), in1=x_n, op=ALU.add)
+                st["a", k, t] = a_t
+
         def th(k, t):
-            cnd = work.tile([P, C], F32, name="cnd", tag="cnd", bufs=5)
+            cnd = work.tile([P, C], F32, name="cnd", tag="cnd", bufs=6)
+            if x_on_vector(k, t):
+                nc.scalar.activation(out=cnd[:], in_=st["a", k, t][:], func=FN.Tanh)
+                st["c", k, t] = cnd
+                return
             nc.scalar.activation(
                 out=cnd[:].rearrange("n (u p e) -> n u p e", u=2, e=2), in_=natural(st["mn", k, t]), func=FN.Tanh
             )
             st["c", k, t] = cnd
 
         def u_(k, t):
-            u_t = work.tile([P, C], F32, name="u_t", tag="u_t", bufs=4)
+            u_t = work.tile([P, C], F32, name="u_t", tag="u_t", bufs=5)
             nc.gpsimd.tensor_tensor(out=u_t[:], in0=h_of(k, t), in1=st["c", k, t][:], op=ALU.subtract)
             st["u", k, t] = u_t
 
@@ -241,12 +260,12 @@ def tile_gatedgraphconvolution_pb_t_kernel(tc, x_proj, annotations, recurrent_ke
             store(k, t)
 
         def th_last(k, t):
-            cnd = work.tile([P, C], F32, name="cnd", tag="cnd", bufs=5)
+            cnd = work.tile([P, C], F32, name="cnd", tag="cnd", bufs=6)
             nc.scalar.activation(out=cnd[:], in_=st["mn", k, t][:], func=FN.Tanh)
             st["c", k, t] = cnd
 
         def zh(k, t):
-            w = work.tile([P, C], F32, name="zh", tag="u_t", bufs=4)
+            w = work.tile([P, C], F32, name="zh", tag="u_t", bufs=5)
             nc.vector.tensor_tensor(
                 out=w[:].rearrange("n (u e p) -> n u e p", u=2, e=2),
                 in0=st["zn", k, t][:].rearrange("n (u e p) -> n u e p", u=2, e=2),
@@ -304,46 +323,46 @@ def tile_gatedgraphconvolution_pb_t_kernel(tc, x_proj, annotations, recurrent_ke
         load_x_gate(0, RG)
         load_w(CG)
         load_w(ZG)
-        load_x_gate(0, ZG)
-        load_x_gate(0, CG)
         load_h(1)
+        load_x_gate(0, ZG)
         load_x_gate(1, RG)
         load_x_gate(1, ZG)
+        load_x_gate(0, CG)
         load_x_gate(1, CG)
-        for t in range(TILES[0]):
-            ht(0, t)
-            ev(0, t)
-        regroup_w(RG, 0, nc.vector.tensor_copy)
-        for t in range(TILES[0]):
-            q(0, t)
-        quantise_w(RG, 0)
-        regroup_w(RG, 1, nc.vector.tensor_copy)
-        quantise_w(RG, 1)
-        for u in range(2):
-            xw(0, RG, u)
-            xe(0, RG, u)
-        mx(0, RG, 0)
-        nc.vector.tensor_copy(out=b_rows32[:], in_=b_rows[:].rearrange("j (p e) -> j e p", e=2))
-        b_ps = psum.tile([P, C], F32, name="b_ps", tag="zn")
-        for e in range(2):
-            nc.tensor.transpose(b_ps[:, P * e : P * e + P], b_rows32[:, e, :], ident[:])
-        regroup_w(CG, 0, nc.vector.tensor_copy)
-        nc.vector.tensor_copy(out=b_col[:], in_=b_ps[:, 0 : 2 * P].rearrange("p (e j) -> p e j", e=2)[:, :, 0:6])
-        quantise_w(CG, 0)
-        regroup_w(CG, 1, nc.scalar.copy)
-        mx(0, CG, 0)
-        regroup_w(ZG, 0, nc.vector.tensor_copy)
-        quantise_w(ZG, 0)
-        regroup_w(ZG, 1, nc.scalar.copy)
-        quantise_w(CG, 1)
-        quantise_w(ZG, 1)
-        for u in range(2):
-            xw(0, ZG, u)
-            xe(0, ZG, u)
-        mx(0, ZG, 0)
-
-        ht(1, 0)
-        ev(1, 0)
+        with tc.manual_schedule():
+            nc.vector.tensor_copy(out=b_rows32[:], in_=b_rows[:].rearrange("j (p e) -> j e p", e=2))
+            b_ps = psum.tile([P, C], F32, name="b_ps", tag="bank", bufs=8)
+            for e in range(2):
+                nc.tensor.transpose(b_ps[:, P * e : P * e + P], b_rows32[:, e, :], ident[:])
+            nc.vector.tensor_copy(out=b_col[:], in_=b_ps[:, 0 : 2 * P].rearrange("p (e j) -> p e j", e=2)[:, :, 0:6])
+            for t in range(TILES[0]):
+                ht(0, t)
+                ev(0, t)
+            regroup_w(RG, 0, nc.vector.tensor_copy)
+            for t in range(TILES[0]):
+                q(0, t)
+            quantise_w(RG, 0)
+            regroup_w(RG, 1, nc.vector.tensor_copy)
+            regroup_w(CG, 0, nc.vector.tensor_copy)
+            quantise_w(RG, 1)
+            for u in range(2):
+                xw(0, RG, u)
+                xe(0, RG, u)
+            mx(0, RG, 0)
+            regroup_w(ZG, 0, nc.vector.tensor_copy)
+            quantise_w(CG, 0)
+            regroup_w(CG, 1, nc.scalar.copy)
+            mx(0, CG, 0)
+            ht(1, 0)
+            regroup_w(ZG, 1, nc.scalar.copy)
+            ev(1, 0)
+            quantise_w(CG, 1)
+            quantise_w(ZG, 0)
+            quantise_w(ZG, 1)
+            for u in range(2):
+                xw(0, ZG, u)
+                xe(0, ZG, u)
+            mx(0, ZG, 0)
 
         for s in range(NSTEP):
             k1, j = s // NF + 1, s % NF
@@ -353,11 +372,12 @@ def tile_gatedgraphconvolution_pb_t_kernel(tc, x_proj, annotations, recurrent_ke
                 load_x(k1 + 1)
             chunk(add_x, s, RG)
             chunk(add_x, s, ZG)
+            tile_step(ax, s - 1)
             next_h(q, s)
-            tile_step(th, s - 1)
             chunk(sigmoid, s, RG)
-            tile_step(v, s - 2)
-            tile_step(u_, s - 1)
+            tile_step(th, s - 1)
+            tile_step(v, s - 3)
+            tile_step(u_, s - 2)
             if k1 < NBLK:
                 xw(k1, xg, xu)
             next_h(ht, s + 1)
@@ -366,15 +386,19 @@ def tile_gatedgraphconvolution_pb_t_kernel(tc, x_proj, annotations, recurrent_ke
             chunk(mx, s + 1, RG)
             chunk(mx, s + 1, ZG)
             tile_step(mn, s)
-            tile_step(zn, s - 1)
+            tile_step(zn, s - 2)
             chunk(sigmoid, s, ZG)
             if k1 < NBLK:
                 xe(k1, xg, xu)
             next_h(ev, s + 1)
             chunk(m, s)
-            tile_step(o, s - 2)
+            tile_step(o, s - 3)
 
         last = NBLK - 1
+        u_(last - 1, 2)
+        v(last - 1, 1)
+        o(last - 1, 1)
+        zn(last - 1, 2)
         th_last(last - 1, 3)
         v(last - 1, 2)
         o(last - 1, 2)

@@ -32,6 +32,7 @@ def tile_gatedgraphconvolution_pb_t_kernel(tc, x_proj, annotations, recurrent_ke
     out_all = out.flatten_outer_dims()
 
     with ExitStack() as ctx:
+        ctx.enter_context(tc.manual_schedule())
         const = ctx.enter_context(tc.tile_pool(name="const", bufs=1))
         xpool = ctx.enter_context(tc.tile_pool(name="xpool", bufs=4))
         hpool = ctx.enter_context(tc.tile_pool(name="hpool", bufs=5))
@@ -107,8 +108,8 @@ def tile_gatedgraphconvolution_pb_t_kernel(tc, x_proj, annotations, recurrent_ke
 
         def q(k, t):
             if t == 0:
-                st["hc", k] = qpool.tile([P, P * TILES[k]], U32, name="h_codes", tag="h_codes", align_bytes=64)
-                st["hs", k] = qpool.tile([P, P * TILES[k]], U8, name="h_scales", tag="h_scales", align_bytes=64)
+                st["hc", k] = qpool.tile([P, P * TILES[k]], U32, name="h_codes", tag="h_codes", bufs=3, align_bytes=64)
+                st["hs", k] = qpool.tile([P, P * TILES[k]], U8, name="h_scales", tag="h_scales", bufs=3, align_bytes=64)
             ns = slice(P * t, P * t + P)
             nc.vector.quantize_mx(
                 out=st["hc", k][:, ns].bitcast(FP8X4), scales=st["hs", k][:, ns], in_=st["grp", k, t][:]
@@ -329,40 +330,42 @@ def tile_gatedgraphconvolution_pb_t_kernel(tc, x_proj, annotations, recurrent_ke
         load_x_gate(1, ZG)
         load_x_gate(0, CG)
         load_x_gate(1, CG)
-        with tc.manual_schedule():
-            nc.vector.tensor_copy(out=b_rows32[:], in_=b_rows[:].rearrange("j (p e) -> j e p", e=2))
-            b_ps = psum.tile([P, C], F32, name="b_ps", tag="bank", bufs=8)
-            for e in range(2):
-                nc.tensor.transpose(b_ps[:, P * e : P * e + P], b_rows32[:, e, :], ident[:])
-            nc.vector.tensor_copy(out=b_col[:], in_=b_ps[:, 0 : 2 * P].rearrange("p (e j) -> p e j", e=2)[:, :, 0:6])
-            for t in range(TILES[0]):
-                ht(0, t)
-                ev(0, t)
-            regroup_w(RG, 0, nc.vector.tensor_copy)
-            for t in range(TILES[0]):
-                q(0, t)
-            quantise_w(RG, 0)
-            regroup_w(RG, 1, nc.vector.tensor_copy)
-            regroup_w(CG, 0, nc.vector.tensor_copy)
-            quantise_w(RG, 1)
-            for u in range(2):
-                xw(0, RG, u)
-                xe(0, RG, u)
-            mx(0, RG, 0)
-            regroup_w(ZG, 0, nc.vector.tensor_copy)
-            quantise_w(CG, 0)
-            regroup_w(CG, 1, nc.scalar.copy)
-            mx(0, CG, 0)
-            ht(1, 0)
-            regroup_w(ZG, 1, nc.scalar.copy)
-            ev(1, 0)
-            quantise_w(CG, 1)
-            quantise_w(ZG, 0)
-            quantise_w(ZG, 1)
-            for u in range(2):
-                xw(0, ZG, u)
-                xe(0, ZG, u)
-            mx(0, ZG, 0)
+        nc.vector.tensor_copy(out=b_rows32[:], in_=b_rows[:].rearrange("j (p e) -> j e p", e=2))
+        b_ps = psum.tile([P, C], F32, name="b_ps", tag="bank", bufs=8)
+        for e in range(2):
+            nc.tensor.transpose(b_ps[:, P * e : P * e + P], b_rows32[:, e, :], ident[:])
+        nc.vector.tensor_copy(out=b_col[:], in_=b_ps[:, 0 : 2 * P].rearrange("p (e j) -> p e j", e=2)[:, :, 0:6])
+        for t in range(TILES[0]):
+            ht(0, t)
+            ev(0, t)
+        regroup_w(RG, 0, nc.vector.tensor_copy)
+        for t in range(TILES[0]):
+            q(0, t)
+        quantise_w(RG, 0)
+        regroup_w(RG, 1, nc.vector.tensor_copy)
+        regroup_w(CG, 0, nc.vector.tensor_copy)
+        quantise_w(RG, 1)
+        for u in range(2):
+            xw(0, RG, u)
+            xe(0, RG, u)
+        mx(0, RG, 0)
+        regroup_w(ZG, 0, nc.vector.tensor_copy)
+        quantise_w(CG, 0)
+        regroup_w(CG, 1, nc.scalar.copy)
+        mx(0, CG, 0)
+        ht(1, 0)
+        regroup_w(ZG, 1, nc.scalar.copy)
+        ev(1, 0)
+        quantise_w(CG, 1)
+        quantise_w(ZG, 0)
+        quantise_w(ZG, 1)
+        for u in range(2):
+            xw(0, ZG, u)
+            xe(0, ZG, u)
+        mx(0, ZG, 0)
+        ht(1, 1)
+        ev(1, 1)
+        q(1, 0)
 
         for s in range(NSTEP):
             k1, j = s // NF + 1, s % NF
@@ -370,63 +373,59 @@ def tile_gatedgraphconvolution_pb_t_kernel(tc, x_proj, annotations, recurrent_ke
             if j == 0 and k1 + 1 < NBLK:
                 load_h(k1 + 1)
                 load_x(k1 + 1)
-            chunk(add_x, s, RG)
-            chunk(add_x, s, ZG)
-            tile_step(ax, s - 1)
-            next_h(q, s)
-            chunk(sigmoid, s, RG)
-            tile_step(th, s - 1)
-            tile_step(v, s - 3)
-            tile_step(u_, s - 2)
-            if k1 < NBLK:
-                xw(k1, xg, xu)
-            next_h(ht, s + 1)
+            chunk(mx, s + 1, ZG)
             if s > 0:
                 chunk(mx, s, CG)
             chunk(mx, s + 1, RG)
-            chunk(mx, s + 1, ZG)
+            chunk(add_x, s, RG)
+            tile_step(ax, s - 1)
+            chunk(sigmoid, s, RG)
+            tile_step(th, s - 1)
+            if k1 < NBLK:
+                xw(k1, xg, xu)
+            next_h(ht, s + 2)
+            tile_step(zn, s - 1)
             tile_step(mn, s)
-            tile_step(zn, s - 2)
+            chunk(add_x, s, ZG)
             chunk(sigmoid, s, ZG)
+            tile_step(v, s - 2)
+            next_h(q, s + 1)
+            tile_step(u_, s - 1)
+            next_h(ev, s + 2)
             if k1 < NBLK:
                 xe(k1, xg, xu)
-            next_h(ev, s + 1)
             chunk(m, s)
-            tile_step(o, s - 3)
+            tile_step(o, s - 2)
 
         last = NBLK - 1
-        u_(last - 1, 2)
-        v(last - 1, 1)
-        o(last - 1, 1)
-        zn(last - 1, 2)
-        th_last(last - 1, 3)
+        th(last - 1, 3)
         v(last - 1, 2)
+        u_(last - 1, 3)
         o(last - 1, 2)
         mn(last, 0)
         zn(last, 0)
         th_last(last, 0)
         zh(last, 0)
-        zn(last - 1, 3)
         mn(last, 1)
         zn(last, 1)
         th_last(last, 1)
-        zh(last - 1, 3)
         zh(last, 1)
+        zn(last - 1, 3)
         zc(last, 0)
-        zc(last - 1, 3)
+        v(last - 1, 3)
+        o(last - 1, 3)
+        zc(last, 1)
         mn(last, 2)
         zn(last, 2)
         th_last(last, 2)
-        o_last(last, 0, nc.vector)
-        o_last(last - 1, 3, nc.gpsimd)
-        zc(last, 1)
         zh(last, 2)
         mn(last, 3)
         zn(last, 3)
         th_last(last, 3)
-        o_last(last, 1, nc.vector)
-        zc(last, 2)
         zh(last, 3)
-        o_last(last, 2, nc.vector)
+        zc(last, 2)
         zc(last, 3)
+        o_last(last, 0, nc.gpsimd)
+        o_last(last, 1, nc.vector)
+        o_last(last, 2, nc.vector)
         o_last(last, 3, nc.vector)

from contextlib import ExitStack

import concourse.mybir as mybir
from concourse.masks import make_identity

F32 = mybir.dt.float32
BF16 = mybir.dt.bfloat16
U32 = mybir.dt.uint32
U8 = mybir.dt.uint8
I32 = mybir.dt.int32
FP8X4 = mybir.dt.float8_e4m3fn_x4
ALU = mybir.AluOpType
FN = mybir.ActivationFunctionType

P = 128
C = 512
G = 3 * C
R = 4096
NF = C // P
TILES = (4, 4, 4, 4, 4, 4, 4, 4)
FIRST = tuple(sum(TILES[:k]) for k in range(len(TILES)))
NBLK = len(TILES)
NSTEP = NF * NBLK
ZG, RG, CG = 0, 1, 2

FLOPS = 2 * R * C * G


def tile_gatedgraphconvolution_pb_t_kernel(tc, x_proj, annotations, recurrent_kernel, bias_h, out):
    nc = tc.nc
    h_all = annotations.flatten_outer_dims()
    out_all = out.flatten_outer_dims()

    with ExitStack() as ctx:
        ctx.enter_context(tc.manual_schedule())
        const = ctx.enter_context(tc.tile_pool(name="const", bufs=1))
        xpool = ctx.enter_context(tc.tile_pool(name="xpool", bufs=4))
        hpool = ctx.enter_context(tc.tile_pool(name="hpool", bufs=5))
        qpool = ctx.enter_context(tc.tile_pool(name="qpool", bufs=2))
        work = ctx.enter_context(tc.tile_pool(name="work", bufs=3))
        opool = ctx.enter_context(tc.tile_pool(name="opool", bufs=2))
        psum = ctx.enter_context(tc.psum_pool(name="psum", bufs=1))

        h_blks = {}
        x_of = {}
        o_blks = {}
        st = {}

        def rows_of(dram, b):
            rows = slice(P * FIRST[b], P * (FIRST[b] + TILES[b]))
            return dram[rows, :].rearrange("(p t) c -> p t c", t=TILES[b])

        def load_h(b):
            h_blks[b] = hpool.tile([P, TILES[b] * C], BF16, name="h_blk", tag="h_blk")
            nc.sync.dma_start(out=h_blks[b][:], in_=rows_of(h_all, b).rearrange("p t c -> p (t c)"))

        def load_x(b):
            x_blk = xpool.tile([P, TILES[b], G], BF16, name="x_blk", tag="x_blk", align_bytes=64)
            nc.sync.dma_start(out=x_blk[:], in_=rows_of(x_proj, b))
            for g in range(3):
                x_of[b, g] = x_blk[:, :, C * g : C * g + C]

        def load_x_gate(b, g):
            x_g = const.tile([P, TILES[b], C], BF16, name="x_g", tag="x_g%d%d" % (b, g))
            nc.sync.dma_start(out=x_g[:], in_=rows_of(x_proj, b)[:, :, C * g : C * g + C])
            x_of[b, g] = x_g[:]

        def load_w(g):
            nc.sync.dma_start(
                out=w_raw[:, g, :, :],
                in_=recurrent_kernel[:, C * g : C * g + C].rearrange("(q t) c -> q t c", t=4),
            )
            w_codes[g] = const.tile([P, C], U32, name="w_codes", tag="w_codes%d" % g, align_bytes=64)
            w_scales[g] = const.tile([P, C], U8, name="w_scales", tag="w_scales%d" % g, align_bytes=64)

        def regroup_w(g, u, copy):
            cs = slice(256 * u, 256 * u + 256)
            copy(
                out=w_grp[:, g, cs, :].rearrange("q (e p) t -> q e p t", e=2),
                in_=w_raw[:, g, :, cs].rearrange("q t (p e) -> q e p t", e=2),
            )

        def quantise_w(g, u):
            cs = slice(256 * u, 256 * u + 256)
            nc.vector.quantize_mx(
                out=w_codes[g][:, cs].bitcast(FP8X4),
                scales=w_scales[g][:, cs],
                in_=w_grp[:, g, cs, :].rearrange("q c t -> q (c t)"),
            )

        def h_of(k, t):
            return h_blks[k][:, C * t : C * t + C]

        def ht(k, t):
            xt = psum.tile([P, 2, P], F32, name="xt", tag="bank", bufs=8)
            words = h_of(k, t).bitcast(F32)
            for u in range(2):
                nc.tensor.transpose(xt[:, u, :], words[:, u : 2 * P : 2], ident[:])
            st["xt", k, t] = xt

        def ev(k, t):
            h_grp = qpool.tile([P, 4 * P], BF16, name="h_grp", tag="h_grp", bufs=4, align_bytes=64)
            nc.scalar.copy(
                out=h_grp[:].bitcast(F32).rearrange("q (n u) -> q n u", u=2),
                in_=st["xt", k, t][:].rearrange("q u n -> q n u"),
            )
            st["grp", k, t] = h_grp

        def q(k, t):
            if t == 0:
                st["hc", k] = qpool.tile([P, P * TILES[k]], U32, name="h_codes", tag="h_codes", bufs=3, align_bytes=64)
                st["hs", k] = qpool.tile([P, P * TILES[k]], U8, name="h_scales", tag="h_scales", bufs=3, align_bytes=64)
            ns = slice(P * t, P * t + P)
            nc.vector.quantize_mx(
                out=st["hc", k][:, ns].bitcast(FP8X4), scales=st["hs", k][:, ns], in_=st["grp", k, t][:]
            )

        def xw(k, g, u):
            xp = psum.tile([P, P * TILES[k]], F32, name="xp", tag="bank", bufs=8)
            for t in range(TILES[k]):
                words = x_of[k, g][:, t, :].bitcast(F32)
                nc.tensor.transpose(xp[:, P * t : P * t + P], words[:, P * u : P * u + P], ident[:])
            st["xp", k, g, u] = xp

        def xe(k, g, u):
            x_t = work.tile([P, P * TILES[k], 2], BF16, name="x_t", tag="x_t", bufs=8)
            nc.scalar.copy(
                out=x_t[:].rearrange("q n e -> q (n e)").bitcast(F32), in_=st["xp", k, g, u][:]
            )
            st["xT", k, g, u] = x_t

        def mx(k, g, f):
            cs = slice(P * f, P * f + P)
            pg = psum.tile([P, P * TILES[k]], F32, name="pg", tag="bank", bufs=8)
            nc.tensor.matmul_mx(
                out=pg[:],
                lhsT=w_codes[g][:, cs].bitcast(FP8X4),
                lhsT_scale=w_scales[g][:, cs],
                rhs=st["hc", k][:].bitcast(FP8X4),
                rhs_scale=st["hs", k][:],
                start=True,
                stop=True,
            )
            st["p", k, g, f] = pg

        def bias_of(g, f):
            j = 2 * g + f // 2
            return b_col[:, f % 2, j : j + 1]

        def add_x(k, g, f):
            s = work.tile([P, P * TILES[k]], F32, name="s", tag="s%d" % g)
            nc.vector.scalar_tensor_tensor(
                out=s[:],
                in0=st["p", k, g, f][:],
                scalar=bias_of(g, f),
                in1=st["xT", k, g, f // 2][:, :, f % 2],
                op0=ALU.add,
                op1=ALU.add,
            )
            st["s", k, g, f] = s

        def sigmoid(k, g, f):
            gate = work.tile([P, P * TILES[k]], F32, name="gate", tag="g%d" % g, bufs=3 if g == RG else 11)
            nc.scalar.activation(out=gate[:], in_=st["s", k, g, f][:], func=FN.Sigmoid)
            st["g", k, g, f] = gate

        def m(k, f):
            m_t = work.tile([P, P * TILES[k]], F32, name="m_t", tag="m_t", bufs=9)
            nc.vector.scalar_tensor_tensor(
                out=m_t[:],
                in0=st["p", k, CG, f][:],
                scalar=bias_of(CG, f),
                in1=st["g", k, RG, f][:],
                op0=ALU.add,
                op1=ALU.mult,
            )
            st["m", k, f] = m_t

        def zn(k, t):
            ps = psum.tile([P, C], F32, name="zn", tag="bank", bufs=8)
            for f in range(4):
                fs = slice(P * f, P * f + P)
                nc.tensor.transpose(ps[:, fs], st["g", k, ZG, f][:, P * t : P * t + P], ident[:])
            st["zn", k, t] = ps

        def x_on_vector(k, t):
            return t in (0, 2) and k < NBLK - 1

        def mn(k, t):
            ps = psum.tile([P, C], F32, name="mn", tag="bank", bufs=8)
            x_h = x_of[k, CG][:, t, :]
            if x_on_vector(k, t):
                for f in range(NF):
                    nc.tensor.transpose(ps[:, P * f : P * f + P], st["m", k, f][:, P * t : P * t + P], ident[:])
                st["mn", k, t] = ps
                return
            nc.tensor.matmul(
                out=ps[:].rearrange("n (u e p) -> n u e p", u=2, e=2),
                lhsT=ident_bf[:],
                rhs=x_h.rearrange("n (u p e) -> n u e p", u=2, e=2),
                start=True,
                stop=False,
            )
            for f in range(4):
                fs = slice(P * f, P * f + P)
                nc.tensor.matmul(
                    out=ps[:, fs],
                    lhsT=st["m", k, f][:, P * t : P * t + P],
                    rhs=ident[:],
                    is_transpose=True,
                    start=False,
                    stop=(f == 3),
                )
            st["mn", k, t] = ps

        def natural(ps):
            return ps[:].rearrange("n (u e p) -> n u p e", u=2, e=2)

        def ax(k, t):
            if x_on_vector(k, t):
                a_t = work.tile([P, C], F32, name="a_t", tag="a_t", bufs=2)
                a_n = a_t[:].rearrange("n (u p e) -> n u p e", u=2, e=2)
                x_n = x_of[k, CG][:, t, :].rearrange("n (u p e) -> n u p e", u=2, e=2)
                nc.vector.tensor_tensor(out=a_n, in0=natural(st["mn", k, t]), in1=x_n, op=ALU.add)
                st["a", k, t] = a_t

        def th(k, t):
            cnd = work.tile([P, C], F32, name="cnd", tag="cnd", bufs=6)
            if x_on_vector(k, t):
                nc.scalar.activation(out=cnd[:], in_=st["a", k, t][:], func=FN.Tanh)
                st["c", k, t] = cnd
                return
            nc.scalar.activation(
                out=cnd[:].rearrange("n (u p e) -> n u p e", u=2, e=2), in_=natural(st["mn", k, t]), func=FN.Tanh
            )
            st["c", k, t] = cnd

        def u_(k, t):
            u_t = work.tile([P, C], F32, name="u_t", tag="u_t", bufs=5)
            nc.gpsimd.tensor_tensor(out=u_t[:], in0=h_of(k, t), in1=st["c", k, t][:], op=ALU.subtract)
            st["u", k, t] = u_t

        def v(k, t):
            u_n = st["u", k, t][:].rearrange("n (u p e) -> n u p e", u=2, e=2)
            nc.vector.tensor_tensor(out=u_n, in0=natural(st["zn", k, t]), in1=u_n, op=ALU.mult)

        def store(k, t):
            dst = rows_of(out_all, k)
            if k == NBLK - 1:
                nc.sync.dma_start(out=dst[:, t, :], in_=o_blks[k][:, t, :])
            elif t == TILES[k] - 1:
                nc.sync.dma_start(out=dst, in_=o_blks[k][:])

        def o_of(k, t):
            if t == 0:
                o_blks[k] = opool.tile([P, TILES[k], C], F32, name="o_blk", tag="o_blk")
            return o_blks[k][:, t, :]

        def o(k, t):
            nc.gpsimd.tensor_tensor(out=o_of(k, t), in0=st["u", k, t][:], in1=st["c", k, t][:], op=ALU.add)
            store(k, t)

        def th_last(k, t):
            cnd = work.tile([P, C], F32, name="cnd", tag="cnd", bufs=6)
            nc.scalar.activation(out=cnd[:], in_=st["mn", k, t][:], func=FN.Tanh)
            st["c", k, t] = cnd

        def zh(k, t):
            w = work.tile([P, C], F32, name="zh", tag="u_t", bufs=5)
            nc.vector.tensor_tensor(
                out=w[:].rearrange("n (u e p) -> n u e p", u=2, e=2),
                in0=st["zn", k, t][:].rearrange("n (u e p) -> n u e p", u=2, e=2),
                in1=h_of(k, t).rearrange("n (u p e) -> n u e p", u=2, e=2),
                op=ALU.mult,
            )
            st["u", k, t] = w

        def zc(k, t):
            c_t = st["c", k, t]
            nc.vector.scalar_tensor_tensor(
                out=c_t[:], in0=st["zn", k, t][:], scalar=1.0, in1=c_t[:], op0=ALU.subtract, op1=ALU.mult
            )

        def o_last(k, t, engine):
            engine.tensor_tensor(
                out=o_of(k, t).rearrange("n (u p e) -> n u p e", u=2, e=2),
                in0=natural(st["u", k, t]),
                in1=natural(st["c", k, t]),
                op=ALU.subtract,
            )
            store(k, t)

        def chunk(stage, s, *args):
            if 0 <= s < NSTEP:
                stage(s // NF, *args, s % NF)

        def next_h(stage, s):
            k, t = divmod(s, NF)
            if k + 1 < NBLK and t < TILES[k + 1]:
                stage(k + 1, t)

        def tile_step(stage, s):
            k, t = divmod(s - NF, NF)
            if 0 <= k < NBLK and t < TILES[k]:
                stage(k, t)

        w_codes, w_scales = {}, {}
        w_raw = xpool.tile([P, 3, 4, C], BF16, name="w_raw", tag="x_blk", align_bytes=64)
        w_grp = xpool.tile([P, 3, C, 4], BF16, name="w_grp", tag="x_blk", align_bytes=64)
        b_rows = const.tile([P, 2 * P], BF16)
        nc.vector.memset(b_rows[:].bitcast(I32), 0)
        ident = const.tile([P, P], F32)
        make_identity(nc, ident[:])
        ident_bf = const.tile([P, P], BF16)
        make_identity(nc, ident_bf[:])
        nc.sync.dma_start(out=b_rows[0:6, :], in_=bias_h.rearrange("(j q) -> j q", q=2 * P))
        warm = const.tile([P, 1], F32)
        nc.vector.memset(warm[:], 0.0)
        nc.scalar.activation(out=warm[:], in_=warm[:], func=FN.Sigmoid)
        b_rows32 = const.tile([P, 2, P], F32)
        b_col = const.tile([P, 2, 6], F32)
        load_h(0)
        load_w(RG)
        load_x_gate(0, RG)
        load_w(CG)
        load_w(ZG)
        load_h(1)
        load_x_gate(0, ZG)
        load_x_gate(1, RG)
        load_x_gate(1, ZG)
        load_x_gate(0, CG)
        load_x_gate(1, CG)
        nc.vector.tensor_copy(out=b_rows32[:], in_=b_rows[:].rearrange("j (p e) -> j e p", e=2))
        b_ps = psum.tile([P, C], F32, name="b_ps", tag="bank", bufs=8)
        for e in range(2):
            nc.tensor.transpose(b_ps[:, P * e : P * e + P], b_rows32[:, e, :], ident[:])
        nc.vector.tensor_copy(out=b_col[:], in_=b_ps[:, 0 : 2 * P].rearrange("p (e j) -> p e j", e=2)[:, :, 0:6])
        for t in range(TILES[0]):
            ht(0, t)
            ev(0, t)
        regroup_w(RG, 0, nc.vector.tensor_copy)
        for t in range(TILES[0]):
            q(0, t)
        quantise_w(RG, 0)
        regroup_w(RG, 1, nc.vector.tensor_copy)
        regroup_w(CG, 0, nc.vector.tensor_copy)
        quantise_w(RG, 1)
        for u in range(2):
            xw(0, RG, u)
            xe(0, RG, u)
        mx(0, RG, 0)
        regroup_w(ZG, 0, nc.vector.tensor_copy)
        quantise_w(CG, 0)
        regroup_w(CG, 1, nc.scalar.copy)
        mx(0, CG, 0)
        ht(1, 0)
        regroup_w(ZG, 1, nc.scalar.copy)
        ev(1, 0)
        quantise_w(CG, 1)
        quantise_w(ZG, 0)
        quantise_w(ZG, 1)
        for u in range(2):
            xw(0, ZG, u)
            xe(0, ZG, u)
        mx(0, ZG, 0)
        ht(1, 1)
        ev(1, 1)
        q(1, 0)

        for s in range(NSTEP):
            k1, j = s // NF + 1, s % NF
            xg, xu = ((RG, 0), (ZG, 0), (RG, 1), (ZG, 1))[j]
            if j == 0 and k1 + 1 < NBLK:
                load_h(k1 + 1)
                load_x(k1 + 1)
            chunk(mx, s + 1, ZG)
            if s > 0:
                chunk(mx, s, CG)
            chunk(mx, s + 1, RG)
            chunk(add_x, s, RG)
            tile_step(ax, s - 1)
            chunk(sigmoid, s, RG)
            tile_step(th, s - 1)
            if k1 < NBLK:
                xw(k1, xg, xu)
            next_h(ht, s + 2)
            tile_step(zn, s - 1)
            tile_step(mn, s)
            chunk(add_x, s, ZG)
            chunk(sigmoid, s, ZG)
            tile_step(v, s - 2)
            next_h(q, s + 1)
            tile_step(u_, s - 1)
            next_h(ev, s + 2)
            if k1 < NBLK:
                xe(k1, xg, xu)
            chunk(m, s)
            tile_step(o, s - 2)

        last = NBLK - 1
        th(last - 1, 3)
        v(last - 1, 2)
        u_(last - 1, 3)
        o(last - 1, 2)
        mn(last, 0)
        zn(last, 0)
        th_last(last, 0)
        zh(last, 0)
        mn(last, 1)
        zn(last, 1)
        th_last(last, 1)
        zh(last, 1)
        zn(last - 1, 3)
        zc(last, 0)
        v(last - 1, 3)
        o(last - 1, 3)
        zc(last, 1)
        mn(last, 2)
        zn(last, 2)
        th_last(last, 2)
        zh(last, 2)
        mn(last, 3)
        zn(last, 3)
        th_last(last, 3)
        zh(last, 3)
        zc(last, 2)
        zc(last, 3)
        o_last(last, 0, nc.gpsimd)
        o_last(last, 1, nc.vector)
        o_last(last, 2, nc.vector)
        o_last(last, 3, nc.vector)
